import numpy as np
import ml_dtypes


def mxq(x, axis, fmt="e4m3"):
    dtype, down = {"e4m3": (ml_dtypes.float8_e4m3fn, 7), "e5m2": (ml_dtypes.float8_e5m2, 14)}[fmt]
    v = np.moveaxis(np.asarray(x, np.float32).astype(ml_dtypes.bfloat16).astype(np.float64), axis, -1)
    blocks = v.reshape(v.shape[:-1] + (-1, 32))
    amax = np.abs(blocks).max(-1, keepdims=True)
    byte = np.maximum(np.where(amax > 0, np.frexp(amax)[1] - 1 + 127, 0) - down, 1)
    scale = np.exp2(byte - 127.0)
    codes = (blocks / scale).astype(np.float32).astype(dtype).astype(np.float64)
    return np.moveaxis((codes * scale).reshape(v.shape), -1, axis)


WIDE = False


def mx_kscale(k):
    if not WIDE:
        return np.ones(k)
    levels = np.array([10, -10, 5, -5, 0])
    a = np.random.permutation(np.resize(levels, k // 512 * 4)).reshape(k // 512, 4)
    idx = np.arange(k)
    return np.exp2(a[idx // 512, idx % 128 // 32])


BF16 = ml_dtypes.bfloat16


def bf(x):
    return np.asarray(x, np.float32).astype(BF16)


def f64(x):
    return np.asarray(x).astype(np.float64)


B, S, D, F, G, K = 2, 2048, 512, 128, 5, 3
N = B * S
NB = G + K
C = D * NB


def silu(v):
    e = np.exp(-np.abs(v))
    return v * np.where(v >= 0, 1.0, e) / (1.0 + e)


def b_splines(x, grid, k):
    x = x[..., None]
    bases = np.where((x >= grid[:-1]) & (x < grid[1:]), 1.0, 0.0)
    for j in range(1, k + 1):
        left = (x - grid[: -(j + 1)]) / (grid[j:-1] - grid[: -(j + 1)])
        right = (grid[j + 1:] - x) / (grid[j + 1:] - grid[1:-j])
        bases = left * bases[..., :-1] + right * bases[..., 1:]
    return bases


def setup_inputs():
    t = np.maximum(mx_kscale(D), 1.0) ** 2
    return {"x": bf(np.random.standard_normal((B, S, D)) * t),
            "grid": bf(np.arange(-K, G + K + 1) * (2.0 / G) - 1.0),
            "w1_base": bf(np.random.standard_normal((F, D)) / np.sqrt(D) / t),
            "w1_spline": bf(np.random.standard_normal((F, D, NB)) / np.sqrt(D))}


def reference(x, grid, w1_base, w1_spline):
    xf = f64(x).reshape(N, D)
    base = mxq(silu(xf), 1, "e4m3") @ mxq(f64(w1_base), 1, "e4m3").T
    bases = b_splines(xf, f64(grid), K).reshape(N, C)
    spline = mxq(bases, 1, "e4m3") @ mxq(f64(w1_spline).reshape(F, C), 1, "e4m3").T
    return base + spline

@@ -1,0 +1,299 @@
+from contextlib import ExitStack
+
+import concourse.mybir as mybir
+from concourse.masks import make_identity
+
+F32 = mybir.dt.float32
+BF16 = mybir.dt.bfloat16
+U32 = mybir.dt.uint32
+U8 = mybir.dt.uint8
+FP8X4 = mybir.dt.float8_e4m3fn_x4
+ACT = mybir.ActivationFunctionType
+ALU = mybir.AluOpType
+
+P = 128
+PACK = 4
+ROWS = 4096
+FEATURES = P * PACK
+OUT_F = 128
+DEGREE = 3
+KNOTS = 12
+BASES = KNOTS - DEGREE - 1
+PASSES = BASES + 1
+SILU_PASS = BASES
+ROW_TILES = 4
+CHUNK_ROWS = ROW_TILES * P
+CHUNKS = ROWS // CHUNK_ROWS
+PLANE = CHUNK_ROWS * PACK
+STEPS = CHUNKS * KNOTS
+
+FLOPS = 2 * ROWS * OUT_F * (FEATURES + FEATURES * BASES)
+
+
+def tile_kanblock_pa_t_kernel(tc, x, grid, w1_base, w1_spline, out):
+    nc = tc.nc
+    xf = x.flatten_outer_dims()
+
+    with ExitStack() as ctx:
+        ctx.enter_context(tc.manual_schedule())
+        consts = ctx.enter_context(tc.tile_pool(name="consts", bufs=1))
+        work = ctx.enter_context(tc.tile_pool(name="work", bufs=2))
+        psum_turn = ctx.enter_context(tc.psum_pool(name="psum_turn", bufs=4))
+        psum_out = ctx.enter_context(tc.psum_pool(name="psum_out", bufs=2))
+
+        identity = consts.tile([P, P], BF16, name="identity")
+        make_identity(nc, identity[:])
+
+        def features_to_partitions(rows, grouped):
+            turned = psum_turn.tile([P, PACK, P], BF16, name="turned", tag="turned")
+            for t in range(PACK):
+                nc.tensor.transpose(turned[:, t, :], rows[:, t * P : (t + 1) * P], identity[:])
+            nc.scalar.copy(out=grouped, in_=turned[:].rearrange("p t r -> p r t"))
+
+        knot_bf = consts.tile([P, KNOTS], BF16, name="knot_bf")
+        nc.sync.dma_start(out=knot_bf[:], in_=grid.partition_broadcast(P))
+        knot = consts.tile([P, KNOTS], F32, name="knot")
+        nc.vector.tensor_copy(out=knot[:], in_=knot_bf[:])
+        neg_knot = consts.tile([P, KNOTS], F32, name="neg_knot")
+        nc.vector.tensor_scalar_mul(out=neg_knot[:], in0=knot[:], scalar1=-1.0)
+
+        span = {}
+        for k in range(1, DEGREE + 2):
+            span[k] = consts.tile([P, KNOTS - k], F32, name="span%d" % k)
+            nc.vector.tensor_sub(out=span[k][:], in0=knot[:, k:KNOTS], in1=knot[:, 0 : KNOTS - k])
+
+        def spans(k, first):
+            return span[k][:, first : first + BASES]
+
+        def one_over_product(name, factors):
+            result = consts.tile([P, BASES], F32, name=name)
+            nc.vector.tensor_mul(out=result[:], in0=factors[0], in1=factors[1])
+            for factor in factors[2:]:
+                nc.vector.tensor_mul(out=result[:], in0=result[:], in1=factor)
+            nc.vector.reciprocal(out=result[:], in_=result[:])
+            return result
+
+        a_left = one_over_product("a_left", [spans(1, 0), spans(2, 0), spans(3, 0)])
+        b_left = one_over_product("b_left", [spans(1, 0), spans(1, 1), spans(2, 1), spans(3, 1)])
+        nc.vector.tensor_mul(out=b_left[:], in0=b_left[:], in1=spans(4, 0))
+        c_right = one_over_product("c_right", [spans(1, 3), spans(2, 2), spans(3, 1)])
+        d_right = one_over_product("d_right", [spans(1, 3), spans(1, 2), spans(2, 1), spans(3, 0)])
+        nc.vector.tensor_mul(out=d_right[:], in0=d_right[:], in1=spans(4, 0))
+
+        rising_scale = consts.tile([P, BASES + 1], F32, name="rising_scale")
+        nc.vector.tensor_copy(out=rising_scale[:, 0:1], in_=a_left[:, 0:1])
+        nc.vector.tensor_copy(out=rising_scale[:, 1 : BASES + 1], in_=b_left[:])
+        falling_scale = consts.tile([P, BASES + 1], F32, name="falling_scale")
+        nc.vector.tensor_copy(out=falling_scale[:, 0:BASES], in_=d_right[:])
+        nc.vector.tensor_copy(out=falling_scale[:, BASES : BASES + 1], in_=c_right[:, BASES - 1 : BASES])
+        left_ratio = consts.tile([P, BASES], F32, name="left_ratio")
+        nc.vector.reciprocal(out=left_ratio[:], in_=rising_scale[:, 0:BASES])
+        nc.vector.tensor_mul(out=left_ratio[:], in0=left_ratio[:], in1=a_left[:])
+        right_ratio = consts.tile([P, BASES], F32, name="right_ratio")
+        nc.vector.reciprocal(out=right_ratio[:], in_=falling_scale[:, 1 : BASES + 1])
+        nc.vector.tensor_mul(out=right_ratio[:], in0=right_ratio[:], in1=c_right[:])
+        neg_falling_scale = consts.tile([P, BASES + 1], F32, name="neg_falling_scale")
+        nc.vector.tensor_scalar_mul(out=neg_falling_scale[:], in0=falling_scale[:], scalar1=-1.0)
+
+        spline_rows = consts.tile([P, FEATURES * BASES], BF16, name="spline_rows")
+        weight_rows = consts.tile([P, PASSES, FEATURES], BF16, name="weight_rows")
+        weight_grouped = consts.tile([P, PASSES, OUT_F, PACK], BF16, name="weight_grouped", align_bytes=64)
+        weight_codes = consts.tile([P, PASSES, OUT_F], U32, name="weight_codes", align_bytes=64)
+        weight_scales = consts.tile([P, PASSES, OUT_F], U8, name="weight_scales", align_bytes=64)
+
+        def load_weights():
+            nc.sync.dma_start(out=spline_rows[:], in_=w1_spline.rearrange("f i g -> f (i g)"))
+            nc.sync.dma_start(out=weight_rows[:, SILU_PASS, :], in_=w1_base)
+
+        def turn_weights():
+            nc.vector.tensor_copy(
+                out=weight_rows[:, 0:BASES, :], in_=spline_rows[:].rearrange("f (i g) -> f g i", g=BASES)
+            )
+            for k in range(PASSES):
+                features_to_partitions(weight_rows[:, k, :], weight_grouped[:, k, :, :])
+
+        def quantise_weights():
+            nc.vector.quantize_mx(
+                out=weight_codes[:, 0:BASES, :].rearrange("p k f -> p (k f)").bitcast(FP8X4),
+                scales=weight_scales[:, 0:BASES, :].rearrange("p k f -> p (k f)"),
+                in_=weight_grouped[:, 0:BASES, :, :].rearrange("p k f t -> p (k f t)"),
+            )
+            nc.vector.quantize_mx(
+                out=weight_codes[:, SILU_PASS, :].bitcast(FP8X4),
+                scales=weight_scales[:, SILU_PASS, :],
+                in_=weight_grouped[:, SILU_PASS, :, :].rearrange("p f t -> p (f t)"),
+            )
+
+        x_turned = {}
+        x_clamped = {}
+        silu = {}
+        square = {}
+        cube = {}
+        rising = {}
+        falling = {}
+        left = {}
+        basis = {}
+        codes = {}
+        scales = {}
+        acc = {}
+
+        def turn_chunk(c):
+            x_rows = work.tile([P, ROW_TILES, FEATURES], BF16, name="x_rows", tag="x_rows")
+            nc.sync.dma_start(
+                out=x_rows[:],
+                in_=xf[c * CHUNK_ROWS : (c + 1) * CHUNK_ROWS, :].rearrange("(r p) i -> p r i", p=P),
+            )
+            grouped = work.tile([P, CHUNK_ROWS, PACK], BF16, name="x_turned", tag="x_turned", bufs=1)
+            for r in range(ROW_TILES):
+                features_to_partitions(x_rows[:, r, :], grouped[:, r * P : (r + 1) * P, :])
+            x_turned[c] = grouped[:].rearrange("p n t -> p (n t)")
+            silu[c] = work.tile([P, PLANE], BF16, name="silu", tag="silu", align_bytes=64)
+            nc.scalar.activation(out=silu[c][:], in_=x_turned[c], func=ACT.Silu)
+
+        def clamp_chunk(c):
+            x_clamped[c] = work.tile([P, PLANE], BF16, name="x_clamped", tag="x_clamped")
+            nc.vector.tensor_scalar(
+                out=x_clamped[c][:],
+                in0=x_turned[c],
+                scalar1=knot[:, 0:1],
+                scalar2=knot[:, KNOTS - 1 : KNOTS],
+                op0=ALU.max,
+                op1=ALU.min,
+            )
+
+        def square_step(q):
+            c, j = divmod(q, KNOTS)
+            square[q] = work.tile([P, PLANE], F32, name="square", tag="square")
+            nc.scalar.activation(
+                out=square[q][:], in_=x_clamped[c][:], func=ACT.Square, bias=neg_knot[:, j : j + 1], scale=1.0
+            )
+
+        def cube_step(q):
+            c, j = divmod(q, KNOTS)
+            cube[q] = work.tile([P, PLANE], F32, name="cube", tag="cube")
+            nc.vector.scalar_tensor_tensor(
+                out=cube[q][:],
+                in0=x_clamped[c][:],
+                scalar=knot[:, j : j + 1],
+                in1=square[q][:],
+                op0=ALU.subtract,
+                op1=ALU.mult,
+            )
+
+        def one_sided_step(q):
+            j = q % KNOTS
+            if j <= BASES:
+                rising[q] = work.tile([P, PLANE], F32, name="rising", tag="rising", bufs=3)
+                nc.scalar.activation(
+                    out=rising[q][:], in_=cube[q][:], func=ACT.Relu, scale=rising_scale[:, j : j + 1]
+                )
+            if j >= DEGREE:
+                falling[q] = work.tile([P, PLANE], F32, name="falling", tag="falling", bufs=3)
+                nc.scalar.activation(
+                    out=falling[q][:],
+                    in_=cube[q][:],
+                    func=ACT.Relu,
+                    scale=neg_falling_scale[:, j - DEGREE : j - DEGREE + 1],
+                )
+
+        def combine_step(q):
+            c, j = divmod(q, KNOTS)
+            if 1 <= j <= BASES:
+                m = j - 1
+                left[(c, m)] = work.tile([P, PLANE], BF16, name="left", tag="left", bufs=DEGREE + 1)
+                nc.vector.scalar_tensor_tensor(
+                    out=left[(c, m)][:],
+                    in0=rising[q - 1][:],
+                    scalar=left_ratio[:, m : m + 1],
+                    in1=rising[q][:],
+                    op0=ALU.mult,
+                    op1=ALU.subtract,
+                )
+            if j >= DEGREE + 1:
+                m = j - DEGREE - 1
+                right = work.tile([P, PLANE], BF16, name="right", tag="right")
+                nc.vector.scalar_tensor_tensor(
+                    out=right[:],
+                    in0=falling[q][:],
+                    scalar=right_ratio[:, m : m + 1],
+                    in1=falling[q - 1][:],
+                    op0=ALU.mult,
+                    op1=ALU.subtract,
+                )
+                basis[(c, m)] = work.tile([P, PLANE], BF16, name="basis", tag="basis", bufs=3, align_bytes=64)
+                nc.vector.tensor_tensor(out=basis[(c, m)][:], in0=left[(c, m)][:], in1=right[:], op=ALU.max)
+
+        def quantise_plane(c, k, plane):
+            nc.vector.quantize_mx(
+                out=codes[c][:, k, :].bitcast(FP8X4), scales=scales[c][:, k, :], in_=plane[:]
+            )
+
+        def quantise_step(q):
+            c, j = divmod(q, KNOTS)
+            if j < DEGREE + 1:
+                return
+            m = j - DEGREE - 1
+            if m == 0:
+                codes[c] = work.tile([P, PASSES, CHUNK_ROWS], U32, name="codes", tag="codes", bufs=1, align_bytes=64)
+                scales[c] = work.tile([P, PASSES, CHUNK_ROWS], U8, name="scales", tag="scales", bufs=1, align_bytes=64)
+                quantise_plane(c, SILU_PASS, silu[c])
+            quantise_plane(c, m, basis[(c, m)])
+
+        def multiply_chunk(c):
+            acc[c] = psum_out.tile([P, ROW_TILES, OUT_F], F32, name="acc", tag="acc")
+            for r in range(ROW_TILES):
+                row_cols = slice(r * P, (r + 1) * P)
+                for k in range(PASSES):
+                    nc.tensor.matmul_mx(
+                        out=acc[c][:, r, :],
+                        lhsT=codes[c][:, k, row_cols].bitcast(FP8X4),
+                        lhsT_scale=scales[c][:, k, row_cols],
+                        rhs=weight_codes[:, k, :].bitcast(FP8X4),
+                        rhs_scale=weight_scales[:, k, :],
+                        start=(k == 0),
+                        stop=(k == PASSES - 1),
+                    )
+
+        def store_chunk(c):
+            out_rows = work.tile([P, ROW_TILES, OUT_F], F32, name="out_rows", tag="out_rows")
+            nc.scalar.copy(out=out_rows[:], in_=acc[c][:])
+            nc.sync.dma_start(
+                out=out[c * CHUNK_ROWS : (c + 1) * CHUNK_ROWS, :].rearrange("(r p) f -> p r f", p=P),
+                in_=out_rows[:],
+            )
+
+        TURN_AT = 9
+        CLAMP_AT = 10
+        STORE_LAG = 2
+        TURN_WEIGHTS_AT = 1
+        QUANTISE_WEIGHTS_AT = 3
+
+        def in_range(q):
+            return 0 <= q < STEPS
+
+        turn_chunk(0)
+        load_weights()
+        clamp_chunk(0)
+        for q in range(-1, STEPS + 3 + STORE_LAG):
+            c, j = divmod(q, KNOTS)
+            if q == TURN_WEIGHTS_AT:
+                turn_weights()
+            if q == QUANTISE_WEIGHTS_AT:
+                quantise_weights()
+            if in_range(q) and j == TURN_AT and c + 1 < CHUNKS:
+                turn_chunk(c + 1)
+            if in_range(q + 1):
+                square_step(q + 1)
+            if in_range(q):
+                cube_step(q)
+                one_sided_step(q)
+            if in_range(q - 1):
+                combine_step(q - 1)
+            if in_range(q - 2):
+                quantise_step(q - 2)
+                if (q - 2) % KNOTS == KNOTS - 1:
+                    multiply_chunk((q - 2) // KNOTS)
+            if in_range(q - 2 - STORE_LAG) and (q - 2 - STORE_LAG) % KNOTS == KNOTS - 1:
+                store_chunk((q - 2 - STORE_LAG) // KNOTS)
+            if in_range(q) and j == CLAMP_AT and c + 1 < CHUNKS:
+                clamp_chunk(c + 1)

@@ -26,6 +26,13 @@ CHUNK_ROWS = ROW_TILES * P
 CHUNKS = ROWS // CHUNK_ROWS
 PLANE = CHUNK_ROWS * PACK
 STEPS = CHUNKS * KNOTS
+SQUARE_AHEAD = 2
+COMBINE_LAG = 2
+QUANTISE_LAG = COMBINE_LAG + 1
+STORE_LAG = 2
+CLAMP_AT = KNOTS - SQUARE_AHEAD - 2
+TURN_AT = CLAMP_AT - 1
+WEIGHTS_FROM = 1
 
 FLOPS = 2 * ROWS * OUT_F * (FEATURES + FEATURES * BASES)
 
@@ -96,21 +103,19 @@ def tile_kanblock_pa_t_kernel(tc, x, grid, w1_base, w1_spline, out):
         nc.vector.tensor_scalar_mul(out=neg_falling_scale[:], in0=falling_scale[:], scalar1=-1.0)
 
         spline_rows = consts.tile([P, FEATURES * BASES], BF16, name="spline_rows")
-        weight_rows = consts.tile([P, PASSES, FEATURES], BF16, name="weight_rows")
+        spline_by_basis = spline_rows[:].rearrange("f (i g) -> f g i", g=BASES)
+        base_rows = consts.tile([P, FEATURES], BF16, name="base_rows")
         weight_grouped = consts.tile([P, PASSES, OUT_F, PACK], BF16, name="weight_grouped", align_bytes=64)
         weight_codes = consts.tile([P, PASSES, OUT_F], U32, name="weight_codes", align_bytes=64)
         weight_scales = consts.tile([P, PASSES, OUT_F], U8, name="weight_scales", align_bytes=64)
 
         def load_weights():
             nc.sync.dma_start(out=spline_rows[:], in_=w1_spline.rearrange("f i g -> f (i g)"))
-            nc.sync.dma_start(out=weight_rows[:, SILU_PASS, :], in_=w1_base)
+            nc.sync.dma_start(out=base_rows[:], in_=w1_base)
 
-        def turn_weights():
-            nc.vector.tensor_copy(
-                out=weight_rows[:, 0:BASES, :], in_=spline_rows[:].rearrange("f (i g) -> f g i", g=BASES)
-            )
-            for k in range(PASSES):
-                features_to_partitions(weight_rows[:, k, :], weight_grouped[:, k, :, :])
+        def turn_weight_pass(k):
+            rows = base_rows[:] if k == SILU_PASS else spline_by_basis[:, k, :]
+            features_to_partitions(rows, weight_grouped[:, k, :, :])
 
         def quantise_weights():
             nc.vector.quantize_mx(
@@ -124,6 +129,7 @@ def tile_kanblock_pa_t_kernel(tc, x, grid, w1_base, w1_spline, out):
                 in_=weight_grouped[:, SILU_PASS, :, :].rearrange("p f t -> p (f t)"),
             )
 
+        x_rows = {}
         x_turned = {}
         x_clamped = {}
         silu = {}
@@ -137,15 +143,19 @@ def tile_kanblock_pa_t_kernel(tc, x, grid, w1_base, w1_spline, out):
         scales = {}
         acc = {}
 
-        def turn_chunk(c):
-            x_rows = work.tile([P, ROW_TILES, FEATURES], BF16, name="x_rows", tag="x_rows")
+        def load_chunk(c):
+            x_rows[c] = work.tile([P, ROW_TILES, FEATURES], BF16, name="x_rows", tag="x_rows", bufs=1)
             nc.sync.dma_start(
-                out=x_rows[:],
+                out=x_rows[c][:],
                 in_=xf[c * CHUNK_ROWS : (c + 1) * CHUNK_ROWS, :].rearrange("(r p) i -> p r i", p=P),
             )
+
+        def turn_chunk(c):
             grouped = work.tile([P, CHUNK_ROWS, PACK], BF16, name="x_turned", tag="x_turned", bufs=1)
             for r in range(ROW_TILES):
-                features_to_partitions(x_rows[:, r, :], grouped[:, r * P : (r + 1) * P, :])
+                features_to_partitions(x_rows[c][:, r, :], grouped[:, r * P : (r + 1) * P, :])
+            if c + 1 < CHUNKS:
+                load_chunk(c + 1)
             x_turned[c] = grouped[:].rearrange("p n t -> p (n t)")
             silu[c] = work.tile([P, PLANE], BF16, name="silu", tag="silu", align_bytes=64)
             nc.scalar.activation(out=silu[c][:], in_=x_turned[c], func=ACT.Silu)
@@ -163,14 +173,14 @@ def tile_kanblock_pa_t_kernel(tc, x, grid, w1_base, w1_spline, out):
 
         def square_step(q):
             c, j = divmod(q, KNOTS)
-            square[q] = work.tile([P, PLANE], F32, name="square", tag="square")
+            square[q] = work.tile([P, PLANE], F32, name="square", tag="square", bufs=SQUARE_AHEAD + 1)
             nc.scalar.activation(
                 out=square[q][:], in_=x_clamped[c][:], func=ACT.Square, bias=neg_knot[:, j : j + 1], scale=1.0
             )
 
         def cube_step(q):
             c, j = divmod(q, KNOTS)
-            cube[q] = work.tile([P, PLANE], F32, name="cube", tag="cube")
+            cube[q] = work.tile([P, PLANE], F32, name="cube", tag="cube", bufs=3)
             nc.vector.scalar_tensor_tensor(
                 out=cube[q][:],
                 in0=x_clamped[c][:],
@@ -183,12 +193,12 @@ def tile_kanblock_pa_t_kernel(tc, x, grid, w1_base, w1_spline, out):
         def one_sided_step(q):
             j = q % KNOTS
             if j <= BASES:
-                rising[q] = work.tile([P, PLANE], F32, name="rising", tag="rising", bufs=3)
+                rising[q] = work.tile([P, PLANE], F32, name="rising", tag="rising", bufs=COMBINE_LAG + 2)
                 nc.scalar.activation(
                     out=rising[q][:], in_=cube[q][:], func=ACT.Relu, scale=rising_scale[:, j : j + 1]
                 )
             if j >= DEGREE:
-                falling[q] = work.tile([P, PLANE], F32, name="falling", tag="falling", bufs=3)
+                falling[q] = work.tile([P, PLANE], F32, name="falling", tag="falling", bufs=COMBINE_LAG + 2)
                 nc.scalar.activation(
                     out=falling[q][:],
                     in_=cube[q][:],
@@ -200,7 +210,7 @@ def tile_kanblock_pa_t_kernel(tc, x, grid, w1_base, w1_spline, out):
             c, j = divmod(q, KNOTS)
             if 1 <= j <= BASES:
                 m = j - 1
-                left[(c, m)] = work.tile([P, PLANE], BF16, name="left", tag="left", bufs=DEGREE + 1)
+                left[(c, m)] = work.tile([P, PLANE], BF16, name="left", tag="left", bufs=DEGREE + 2)
                 nc.vector.scalar_tensor_tensor(
                     out=left[(c, m)][:],
                     in0=rising[q - 1][:],
@@ -220,7 +230,7 @@ def tile_kanblock_pa_t_kernel(tc, x, grid, w1_base, w1_spline, out):
                     op0=ALU.mult,
                     op1=ALU.subtract,
                 )
-                basis[(c, m)] = work.tile([P, PLANE], BF16, name="basis", tag="basis", bufs=3, align_bytes=64)
+                basis[(c, m)] = work.tile([P, PLANE], BF16, name="basis", tag="basis", align_bytes=64)
                 nc.vector.tensor_tensor(out=basis[(c, m)][:], in0=left[(c, m)][:], in1=right[:], op=ALU.max)
 
         def quantise_plane(c, k, plane):
@@ -262,38 +272,33 @@ def tile_kanblock_pa_t_kernel(tc, x, grid, w1_base, w1_spline, out):
                 in_=out_rows[:],
             )
 
-        TURN_AT = 9
-        CLAMP_AT = 10
-        STORE_LAG = 2
-        TURN_WEIGHTS_AT = 1
-        QUANTISE_WEIGHTS_AT = 3
-
         def in_range(q):
             return 0 <= q < STEPS
 
-        turn_chunk(0)
+        load_chunk(0)
         load_weights()
+        turn_chunk(0)
         clamp_chunk(0)
-        for q in range(-1, STEPS + 3 + STORE_LAG):
+        for q in range(-SQUARE_AHEAD, STEPS + QUANTISE_LAG + STORE_LAG + 1):
             c, j = divmod(q, KNOTS)
-            if q == TURN_WEIGHTS_AT:
-                turn_weights()
-            if q == QUANTISE_WEIGHTS_AT:
-                quantise_weights()
             if in_range(q) and j == TURN_AT and c + 1 < CHUNKS:
                 turn_chunk(c + 1)
-            if in_range(q + 1):
-                square_step(q + 1)
+            if 0 <= q - WEIGHTS_FROM < PASSES:
+                turn_weight_pass(q - WEIGHTS_FROM)
+            if q == WEIGHTS_FROM + PASSES + 1:
+                quantise_weights()
+            if in_range(q + SQUARE_AHEAD):
+                square_step(q + SQUARE_AHEAD)
             if in_range(q):
                 cube_step(q)
                 one_sided_step(q)
-            if in_range(q - 1):
-                combine_step(q - 1)
-            if in_range(q - 2):
-                quantise_step(q - 2)
-                if (q - 2) % KNOTS == KNOTS - 1:
-                    multiply_chunk((q - 2) // KNOTS)
-            if in_range(q - 2 - STORE_LAG) and (q - 2 - STORE_LAG) % KNOTS == KNOTS - 1:
-                store_chunk((q - 2 - STORE_LAG) // KNOTS)
+            if in_range(q - COMBINE_LAG):
+                combine_step(q - COMBINE_LAG)
+            if in_range(q - QUANTISE_LAG):
+                quantise_step(q - QUANTISE_LAG)
+                if (q - QUANTISE_LAG) % KNOTS == KNOTS - 1:
+                    multiply_chunk((q - QUANTISE_LAG) // KNOTS)
+            if in_range(q - QUANTISE_LAG - STORE_LAG) and (q - QUANTISE_LAG - STORE_LAG) % KNOTS == KNOTS - 1:
+                store_chunk((q - QUANTISE_LAG - STORE_LAG) // KNOTS)
             if in_range(q) and j == CLAMP_AT and c + 1 < CHUNKS:
                 clamp_chunk(c + 1)

@@ -21,18 +21,20 @@ KNOTS = 12
 BASES = KNOTS - DEGREE - 1
 PASSES = BASES + 1
 SILU_PASS = BASES
-ROW_TILES = 4
+GROUP = 4
+ROW_TILES = 2
 CHUNK_ROWS = ROW_TILES * P
 CHUNKS = ROWS // CHUNK_ROWS
-PLANE = CHUNK_ROWS * PACK
+PLANE = ROW_TILES * FEATURES
 STEPS = CHUNKS * KNOTS
+TURN_KNOTS = 3
+STAGES_A_CHUNK = KNOTS // TURN_KNOTS
+BASES_A_STAGE = BASES // STAGES_A_CHUNK
+HALVES = ((0,), (1, 2), (3,))
+LEFT_LAG = 1
+RIGHT_LAG = 2
 SQUARE_AHEAD = 2
-COMBINE_LAG = 2
-QUANTISE_LAG = COMBINE_LAG + 1
-STORE_LAG = 2
-CLAMP_AT = KNOTS - SQUARE_AHEAD - 2
-TURN_AT = CLAMP_AT - 1
-WEIGHTS_FROM = 1
+PSUM_CHUNKS = 14
 
 FLOPS = 2 * ROWS * OUT_F * (FEATURES + FEATURES * BASES)
 
@@ -45,24 +47,45 @@ def tile_kanblock_pa_t_kernel(tc, x, grid, w1_base, w1_spline, out):
         ctx.enter_context(tc.manual_schedule())
         consts = ctx.enter_context(tc.tile_pool(name="consts", bufs=1))
         work = ctx.enter_context(tc.tile_pool(name="work", bufs=2))
-        psum_turn = ctx.enter_context(tc.psum_pool(name="psum_turn", bufs=4))
-        psum_out = ctx.enter_context(tc.psum_pool(name="psum_out", bufs=2))
+        psum = ctx.enter_context(tc.psum_pool(name="psum", bufs=2))
 
         identity = consts.tile([P, P], BF16, name="identity")
         make_identity(nc, identity[:])
+        identity_f32 = consts.tile([P, P], F32, name="identity_f32")
+        make_identity(nc, identity_f32[:])
 
-        def features_to_partitions(rows, grouped):
-            turned = psum_turn.tile([P, PACK, P], BF16, name="turned", tag="turned")
-            for t in range(PACK):
-                nc.tensor.transpose(turned[:, t, :], rows[:, t * P : (t + 1) * P], identity[:])
-            nc.scalar.copy(out=grouped, in_=turned[:].rearrange("p t r -> p r t"))
+        x_rows = {}
+
+        def load_chunk(c):
+            x_rows[c] = work.tile([P, PLANE], BF16, name="x_rows", tag="x_rows", bufs=3)
+            nc.sync.dma_start(
+                out=x_rows[c][:],
+                in_=xf[c * CHUNK_ROWS : (c + 1) * CHUNK_ROWS, :].rearrange("(p r) i -> p (r i)", r=ROW_TILES),
+            )
 
         knot_bf = consts.tile([P, KNOTS], BF16, name="knot_bf")
         nc.sync.dma_start(out=knot_bf[:], in_=grid.partition_broadcast(P))
+        load_chunk(0)
+        load_chunk(1)
         knot = consts.tile([P, KNOTS], F32, name="knot")
         nc.vector.tensor_copy(out=knot[:], in_=knot_bf[:])
         neg_knot = consts.tile([P, KNOTS], F32, name="neg_knot")
         nc.vector.tensor_scalar_mul(out=neg_knot[:], in0=knot[:], scalar1=-1.0)
+
+        x_clamped = {}
+
+        def clamp_chunk(c):
+            x_clamped[c] = work.tile([P, PLANE], BF16, name="x_clamped", tag="x_clamped", bufs=3)
+            nc.vector.tensor_scalar(
+                out=x_clamped[c][:],
+                in0=x_rows[c][:],
+                scalar1=knot[:, 0:1],
+                scalar2=knot[:, KNOTS - 1 : KNOTS],
+                op0=ALU.max,
+                op1=ALU.min,
+            )
+
+        clamp_chunk(0)
 
         span = {}
         for k in range(1, DEGREE + 2):
@@ -72,35 +95,50 @@ def tile_kanblock_pa_t_kernel(tc, x, grid, w1_base, w1_spline, out):
         def spans(k, first):
             return span[k][:, first : first + BASES]
 
-        def one_over_product(name, factors):
+        def product(name, factors):
             result = consts.tile([P, BASES], F32, name=name)
             nc.vector.tensor_mul(out=result[:], in0=factors[0], in1=factors[1])
             for factor in factors[2:]:
                 nc.vector.tensor_mul(out=result[:], in0=result[:], in1=factor)
+            return result
+
+        def reciprocal(result):
             nc.vector.reciprocal(out=result[:], in_=result[:])
             return result
 
-        a_left = one_over_product("a_left", [spans(1, 0), spans(2, 0), spans(3, 0)])
-        b_left = one_over_product("b_left", [spans(1, 0), spans(1, 1), spans(2, 1), spans(3, 1)])
-        nc.vector.tensor_mul(out=b_left[:], in0=b_left[:], in1=spans(4, 0))
-        c_right = one_over_product("c_right", [spans(1, 3), spans(2, 2), spans(3, 1)])
-        d_right = one_over_product("d_right", [spans(1, 3), spans(1, 2), spans(2, 1), spans(3, 0)])
-        nc.vector.tensor_mul(out=d_right[:], in0=d_right[:], in1=spans(4, 0))
+        a_left = reciprocal(product("a_left", [spans(1, 0), spans(2, 0), spans(3, 0)]))
+        c_right = reciprocal(product("c_right", [spans(1, 3), spans(2, 2), spans(3, 1)]))
+        b_over_a = reciprocal(product("b_over_a", [spans(1, 1), spans(2, 1), spans(3, 1)]))
+        b_over_a_top = product("b_over_a_top", [spans(2, 0), spans(3, 0), spans(4, 0)])
+        c_over_d = reciprocal(product("c_over_d", [spans(4, 0), spans(2, 2), spans(3, 1)]))
+        c_over_d_top = product("c_over_d_top", [spans(1, 2), spans(2, 1), spans(3, 0)])
+        ones = consts.tile([P, BASES], F32, name="ones")
+        nc.vector.memset(ones[:], 1.0)
 
-        rising_scale = consts.tile([P, BASES + 1], F32, name="rising_scale")
-        nc.vector.tensor_copy(out=rising_scale[:, 0:1], in_=a_left[:, 0:1])
-        nc.vector.tensor_copy(out=rising_scale[:, 1 : BASES + 1], in_=b_left[:])
-        falling_scale = consts.tile([P, BASES + 1], F32, name="falling_scale")
-        nc.vector.tensor_copy(out=falling_scale[:, 0:BASES], in_=d_right[:])
-        nc.vector.tensor_copy(out=falling_scale[:, BASES : BASES + 1], in_=c_right[:, BASES - 1 : BASES])
-        left_ratio = consts.tile([P, BASES], F32, name="left_ratio")
-        nc.vector.reciprocal(out=left_ratio[:], in_=rising_scale[:, 0:BASES])
-        nc.vector.tensor_mul(out=left_ratio[:], in0=left_ratio[:], in1=a_left[:])
-        right_ratio = consts.tile([P, BASES], F32, name="right_ratio")
-        nc.vector.reciprocal(out=right_ratio[:], in_=falling_scale[:, 1 : BASES + 1])
-        nc.vector.tensor_mul(out=right_ratio[:], in0=right_ratio[:], in1=c_right[:])
-        neg_falling_scale = consts.tile([P, BASES + 1], F32, name="neg_falling_scale")
-        nc.vector.tensor_scalar_mul(out=neg_falling_scale[:], in0=falling_scale[:], scalar1=-1.0)
+        def running_product(name, top, below):
+            nc.vector.scalar_tensor_tensor(
+                out=below[:], in0=below[:], scalar=-1.0, in1=top[:], op0=ALU.mult, op1=ALU.mult
+            )
+            result = consts.tile([P, BASES + 1], F32, name=name)
+            nc.vector.memset(result[:, 0:1], 1.0)
+            nc.vector.tensor_tensor_scan(
+                out=result[:, 1 : BASES + 1], data0=below[:], data1=ones[:], initial=1.0, op0=ALU.mult, op1=ALU.mult
+            )
+            return result
+
+        rising_scale = running_product("rising_scale", b_over_a_top, b_over_a)
+        falling_scale = running_product("falling_scale", c_over_d_top, c_over_d)
+        last = consts.tile([P, 1], F32, name="last")
+        nc.vector.reciprocal(out=last[:], in_=falling_scale[:, BASES : BASES + 1])
+        nc.vector.tensor_scalar_mul(out=falling_scale[:], in0=falling_scale[:], scalar1=last[:])
+        left_scale = consts.tile([P, BASES], F32, name="left_scale")
+        nc.vector.reciprocal(out=left_scale[:], in_=rising_scale[:, 0:BASES])
+        nc.vector.tensor_mul(out=left_scale[:], in0=left_scale[:], in1=a_left[:])
+        right_scale = consts.tile([P, BASES], F32, name="right_scale")
+        nc.vector.reciprocal(out=right_scale[:], in_=falling_scale[:, 1 : BASES + 1])
+        nc.vector.scalar_tensor_tensor(
+            out=right_scale[:], in0=right_scale[:], scalar=-1.0, in1=c_right[:], op0=ALU.mult, op1=ALU.mult
+        )
 
         spline_rows = consts.tile([P, FEATURES * BASES], BF16, name="spline_rows")
         spline_by_basis = spline_rows[:].rearrange("f (i g) -> f g i", g=BASES)
@@ -115,7 +153,10 @@ def tile_kanblock_pa_t_kernel(tc, x, grid, w1_base, w1_spline, out):
 
         def turn_weight_pass(k):
             rows = base_rows[:] if k == SILU_PASS else spline_by_basis[:, k, :]
-            features_to_partitions(rows, weight_grouped[:, k, :, :])
+            turned = psum.tile([P, PACK, P], BF16, name="turned", tag="turned", bufs=1)
+            for t in range(PACK):
+                nc.tensor.transpose(turned[:, t, :], rows[:, t * P : (t + 1) * P], identity[:])
+            nc.scalar.copy(out=weight_grouped[:, k, :, :], in_=turned[:].rearrange("p t r -> p r t"))
 
         def quantise_weights():
             nc.vector.quantize_mx(
@@ -129,9 +170,7 @@ def tile_kanblock_pa_t_kernel(tc, x, grid, w1_base, w1_spline, out):
                 in_=weight_grouped[:, SILU_PASS, :, :].rearrange("p f t -> p (f t)"),
             )
 
-        x_rows = {}
-        x_turned = {}
-        x_clamped = {}
+        x_second = {}
         silu = {}
         square = {}
         cube = {}
@@ -143,114 +182,130 @@ def tile_kanblock_pa_t_kernel(tc, x, grid, w1_base, w1_spline, out):
         scales = {}
         acc = {}
 
-        def load_chunk(c):
-            x_rows[c] = work.tile([P, ROW_TILES, FEATURES], BF16, name="x_rows", tag="x_rows", bufs=1)
-            nc.sync.dma_start(
-                out=x_rows[c][:],
-                in_=xf[c * CHUNK_ROWS : (c + 1) * CHUNK_ROWS, :].rearrange("(r p) i -> p r i", p=P),
-            )
-
-        def turn_chunk(c):
-            grouped = work.tile([P, CHUNK_ROWS, PACK], BF16, name="x_turned", tag="x_turned", bufs=1)
+        def pass_chunk(c):
+            if c >= PSUM_CHUNKS:
+                x_second[c] = x_clamped[c]
+                return
+            x_second[c] = psum.tile([P, PLANE], BF16, name="x_psum", tag="x_psum", bufs=2)
             for r in range(ROW_TILES):
-                features_to_partitions(x_rows[c][:, r, :], grouped[:, r * P : (r + 1) * P, :])
-            if c + 1 < CHUNKS:
-                load_chunk(c + 1)
-            x_turned[c] = grouped[:].rearrange("p n t -> p (n t)")
-            silu[c] = work.tile([P, PLANE], BF16, name="silu", tag="silu", align_bytes=64)
-            nc.scalar.activation(out=silu[c][:], in_=x_turned[c], func=ACT.Silu)
+                cols = slice(r * FEATURES, (r + 1) * FEATURES)
+                nc.tensor.matmul(
+                    out=x_second[c][:, cols], lhsT=identity[:], rhs=x_clamped[c][:, cols], start=True, stop=True
+                )
 
-        def clamp_chunk(c):
-            x_clamped[c] = work.tile([P, PLANE], BF16, name="x_clamped", tag="x_clamped")
-            nc.vector.tensor_scalar(
-                out=x_clamped[c][:],
-                in0=x_turned[c],
-                scalar1=knot[:, 0:1],
-                scalar2=knot[:, KNOTS - 1 : KNOTS],
-                op0=ALU.max,
-                op1=ALU.min,
-            )
+        def silu_chunk(c):
+            turned = psum.tile([P, PACK, CHUNK_ROWS], BF16, name="turned", tag="turned", bufs=1)
+            for r in range(ROW_TILES):
+                for t in range(PACK):
+                    first = r * FEATURES + t * P
+                    nc.tensor.transpose(
+                        turned[:, t, r * P : (r + 1) * P], x_rows[c][:, first : first + P], identity[:]
+                    )
+            silu[c] = work.tile([P, CHUNK_ROWS, PACK], BF16, name="silu", tag="silu", align_bytes=64)
+            nc.scalar.activation(out=silu[c][:], in_=turned[:].rearrange("p t n -> p n t"), func=ACT.Silu)
 
-        def square_step(q):
-            c, j = divmod(q, KNOTS)
-            square[q] = work.tile([P, PLANE], F32, name="square", tag="square", bufs=SQUARE_AHEAD + 1)
+        def square_step(n):
+            c, j = divmod(n, KNOTS)
+            square[n] = work.tile([P, PLANE], F32, name="square", tag="square", bufs=SQUARE_AHEAD + 2)
             nc.scalar.activation(
-                out=square[q][:], in_=x_clamped[c][:], func=ACT.Square, bias=neg_knot[:, j : j + 1], scale=1.0
+                out=square[n][:], in_=x_clamped[c][:], func=ACT.Square, bias=neg_knot[:, j : j + 1], scale=1.0
             )
 
-        def cube_step(q):
-            c, j = divmod(q, KNOTS)
-            cube[q] = work.tile([P, PLANE], F32, name="cube", tag="cube", bufs=3)
+        def cube_step(n):
+            c, j = divmod(n, KNOTS)
+            if j == 0 or j == KNOTS - 1:
+                cube[n] = work.tile([P, PLANE], F32, name="end_cube", tag="end_cube", bufs=3)
+            else:
+                cube[n] = work.tile([P, PLANE], F32, name="cube", tag="cube", bufs=4)
             nc.vector.scalar_tensor_tensor(
-                out=cube[q][:],
-                in0=x_clamped[c][:],
+                out=cube[n][:],
+                in0=x_second[c][:],
                 scalar=knot[:, j : j + 1],
-                in1=square[q][:],
+                in1=square[n][:],
                 op0=ALU.subtract,
                 op1=ALU.mult,
             )
 
-        def one_sided_step(q):
-            j = q % KNOTS
-            if j <= BASES:
-                rising[q] = work.tile([P, PLANE], F32, name="rising", tag="rising", bufs=COMBINE_LAG + 2)
-                nc.scalar.activation(
-                    out=rising[q][:], in_=cube[q][:], func=ACT.Relu, scale=rising_scale[:, j : j + 1]
+        def one_sided_step(n):
+            j = n % KNOTS
+            if j == 0:
+                rising[n] = cube[n]
+            elif j <= BASES:
+                rising[n] = work.tile([P, PLANE], F32, name="rising", tag="rising", bufs=7)
+                nc.gpsimd.tensor_scalar(
+                    out=rising[n][:],
+                    in0=cube[n][:],
+                    scalar1=rising_scale[:, j : j + 1],
+                    scalar2=0.0,
+                    op0=ALU.mult,
+                    op1=ALU.max if j % 2 == 0 else ALU.min,
                 )
-            if j >= DEGREE:
-                falling[q] = work.tile([P, PLANE], F32, name="falling", tag="falling", bufs=COMBINE_LAG + 2)
-                nc.scalar.activation(
-                    out=falling[q][:],
-                    in_=cube[q][:],
-                    func=ACT.Relu,
-                    scale=neg_falling_scale[:, j - DEGREE : j - DEGREE + 1],
+            if j == KNOTS - 1:
+                falling[n] = cube[n]
+            elif j >= DEGREE:
+                falling[n] = work.tile([P, PLANE], F32, name="falling", tag="falling", bufs=7)
+                nc.gpsimd.tensor_scalar(
+                    out=falling[n][:],
+                    in0=cube[n][:],
+                    scalar1=falling_scale[:, j - DEGREE : j - DEGREE + 1],
+                    scalar2=0.0,
+                    op0=ALU.mult,
+                    op1=ALU.min if (KNOTS - 1 - j) % 2 == 0 else ALU.max,
                 )
 
-        def combine_step(q):
-            c, j = divmod(q, KNOTS)
-            if 1 <= j <= BASES:
-                m = j - 1
-                left[(c, m)] = work.tile([P, PLANE], BF16, name="left", tag="left", bufs=DEGREE + 2)
-                nc.vector.scalar_tensor_tensor(
-                    out=left[(c, m)][:],
-                    in0=rising[q - 1][:],
-                    scalar=left_ratio[:, m : m + 1],
-                    in1=rising[q][:],
-                    op0=ALU.mult,
-                    op1=ALU.subtract,
+        def turn_sum(tag, bufs, first, second, r):
+            total = psum.tile([P, PACK, P], F32, name=tag, tag=tag, bufs=bufs)
+            for t in range(PACK):
+                cols = slice(r * FEATURES + t * P, r * FEATURES + (t + 1) * P)
+                nc.tensor.matmul(
+                    out=total[:, t, :], lhsT=first[:, cols], rhs=identity_f32[:], is_transpose=True, start=True, stop=False
                 )
-            if j >= DEGREE + 1:
-                m = j - DEGREE - 1
-                right = work.tile([P, PLANE], BF16, name="right", tag="right")
-                nc.vector.scalar_tensor_tensor(
-                    out=right[:],
-                    in0=falling[q][:],
-                    scalar=right_ratio[:, m : m + 1],
-                    in1=falling[q - 1][:],
-                    op0=ALU.mult,
-                    op1=ALU.subtract,
+                nc.tensor.matmul(
+                    out=total[:, t, :], lhsT=second[:, cols], rhs=identity_f32[:], is_transpose=True, start=False, stop=True
                 )
-                basis[(c, m)] = work.tile([P, PLANE], BF16, name="basis", tag="basis", align_bytes=64)
-                nc.vector.tensor_tensor(out=basis[(c, m)][:], in0=left[(c, m)][:], in1=right[:], op=ALU.max)
+            return total[:].rearrange("p t n -> p n t")
 
-        def quantise_plane(c, k, plane):
-            nc.vector.quantize_mx(
-                out=codes[c][:, k, :].bitcast(FP8X4), scales=scales[c][:, k, :], in_=plane[:]
+        def left_branch(c, m, r):
+            n = c * KNOTS + m
+            total = turn_sum("left_sum", 2, rising[n], rising[n + 1], r)
+            left[(c, m, r)] = work.tile([P, P, PACK], BF16, name="left", tag="left", bufs=10)
+            nc.scalar.activation(out=left[(c, m, r)][:], in_=total, func=ACT.Relu, scale=left_scale[:, m : m + 1])
+
+        def right_branch(c, m, r):
+            n = c * KNOTS + m
+            total = turn_sum("right_sum", 3, falling[n + DEGREE + 1], falling[n + DEGREE], r)
+            group, place = divmod(m, GROUP)
+            if place == 0 and r == 0:
+                basis[(c, group)] = work.tile(
+                    [P, GROUP, CHUNK_ROWS, PACK], BF16, name="basis", tag="basis", bufs=3, align_bytes=64
+                )
+            nc.vector.scalar_tensor_tensor(
+                out=basis[(c, group)][:, place, r * P : (r + 1) * P, :],
+                in0=total,
+                scalar=right_scale[:, m : m + 1],
+                in1=left[(c, m, r)][:],
+                op0=ALU.mult,
+                op1=ALU.max,
             )
 
-        def quantise_step(q):
-            c, j = divmod(q, KNOTS)
-            if j < DEGREE + 1:
-                return
-            m = j - DEGREE - 1
-            if m == 0:
-                codes[c] = work.tile([P, PASSES, CHUNK_ROWS], U32, name="codes", tag="codes", bufs=1, align_bytes=64)
-                scales[c] = work.tile([P, PASSES, CHUNK_ROWS], U8, name="scales", tag="scales", bufs=1, align_bytes=64)
-                quantise_plane(c, SILU_PASS, silu[c])
-            quantise_plane(c, m, basis[(c, m)])
+        def quantise_group(c, group):
+            if group == 0:
+                codes[c] = work.tile([P, PASSES, CHUNK_ROWS], U32, name="codes", tag="codes", align_bytes=64)
+                scales[c] = work.tile([P, PASSES, CHUNK_ROWS], U8, name="scales", tag="scales", align_bytes=64)
+                nc.vector.quantize_mx(
+                    out=codes[c][:, SILU_PASS, :].bitcast(FP8X4),
+                    scales=scales[c][:, SILU_PASS, :],
+                    in_=silu[c][:].rearrange("p n t -> p (n t)"),
+                )
+            planes = slice(group * GROUP, (group + 1) * GROUP)
+            nc.vector.quantize_mx(
+                out=codes[c][:, planes, :].rearrange("p k n -> p (k n)").bitcast(FP8X4),
+                scales=scales[c][:, planes, :].rearrange("p k n -> p (k n)"),
+                in_=basis[(c, group)][:].rearrange("p k n t -> p (k n t)"),
+            )
 
         def multiply_chunk(c):
-            acc[c] = psum_out.tile([P, ROW_TILES, OUT_F], F32, name="acc", tag="acc")
+            acc[c] = psum.tile([P, ROW_TILES, OUT_F], F32, name="acc", tag="turned", bufs=1)
             for r in range(ROW_TILES):
                 row_cols = slice(r * P, (r + 1) * P)
                 for k in range(PASSES):
@@ -268,37 +323,48 @@ def tile_kanblock_pa_t_kernel(tc, x, grid, w1_base, w1_spline, out):
             out_rows = work.tile([P, ROW_TILES, OUT_F], F32, name="out_rows", tag="out_rows")
             nc.scalar.copy(out=out_rows[:], in_=acc[c][:])
             nc.sync.dma_start(
-                out=out[c * CHUNK_ROWS : (c + 1) * CHUNK_ROWS, :].rearrange("(r p) f -> p r f", p=P),
+                out=out[c * CHUNK_ROWS : (c + 1) * CHUNK_ROWS, :].rearrange("(p r) f -> p r f", r=ROW_TILES),
                 in_=out_rows[:],
             )
 
-        def in_range(q):
-            return 0 <= q < STEPS
-
-        load_chunk(0)
         load_weights()
-        turn_chunk(0)
-        clamp_chunk(0)
-        for q in range(-SQUARE_AHEAD, STEPS + QUANTISE_LAG + STORE_LAG + 1):
-            c, j = divmod(q, KNOTS)
-            if in_range(q) and j == TURN_AT and c + 1 < CHUNKS:
-                turn_chunk(c + 1)
-            if 0 <= q - WEIGHTS_FROM < PASSES:
-                turn_weight_pass(q - WEIGHTS_FROM)
-            if q == WEIGHTS_FROM + PASSES + 1:
+        pass_chunk(0)
+        stages = CHUNKS * STAGES_A_CHUNK
+        for n in range(-SQUARE_AHEAD, (stages + 6) * TURN_KNOTS):
+            c, j = divmod(n, KNOTS)
+            stage, part = divmod(n, TURN_KNOTS)
+            if 0 <= n < STEPS and j == 0 and c + 2 < CHUNKS:
+                load_chunk(c + 2)
+            if 0 <= n + SQUARE_AHEAD < STEPS:
+                square_step(n + SQUARE_AHEAD)
+            if 0 <= n < STEPS:
+                cube_step(n)
+                one_sided_step(n)
+            for half in HALVES[part]:
+                base, r = divmod(half, ROW_TILES)
+                q = stage - RIGHT_LAG
+                if 0 <= q < stages:
+                    right_branch(q // STAGES_A_CHUNK, (q % STAGES_A_CHUNK) * BASES_A_STAGE + base, r)
+                q = stage - LEFT_LAG
+                if 0 <= q < stages:
+                    left_branch(q // STAGES_A_CHUNK, (q % STAGES_A_CHUNK) * BASES_A_STAGE + base, r)
+            if 0 <= n < STEPS and j == 1:
+                silu_chunk(c)
+            if 2 <= n < 2 + PASSES:
+                turn_weight_pass(n - 2)
+            if n == KNOTS:
                 quantise_weights()
-            if in_range(q + SQUARE_AHEAD):
-                square_step(q + SQUARE_AHEAD)
-            if in_range(q):
-                cube_step(q)
-                one_sided_step(q)
-            if in_range(q - COMBINE_LAG):
-                combine_step(q - COMBINE_LAG)
-            if in_range(q - QUANTISE_LAG):
-                quantise_step(q - QUANTISE_LAG)
-                if (q - QUANTISE_LAG) % KNOTS == KNOTS - 1:
-                    multiply_chunk((q - QUANTISE_LAG) // KNOTS)
-            if in_range(q - QUANTISE_LAG - STORE_LAG) and (q - QUANTISE_LAG - STORE_LAG) % KNOTS == KNOTS - 1:
-                store_chunk((q - QUANTISE_LAG - STORE_LAG) // KNOTS)
-            if in_range(q) and j == CLAMP_AT and c + 1 < CHUNKS:
-                clamp_chunk(c + 1)
+            q = stage - RIGHT_LAG - 1
+            if part == 1 and 0 <= q < stages and q % 2 == 1:
+                quantise_group(q // STAGES_A_CHUNK, (q % STAGES_A_CHUNK) // 2)
+            q = stage - RIGHT_LAG - 2
+            if 0 <= q < stages and q % STAGES_A_CHUNK == STAGES_A_CHUNK - 1:
+                if part == 0:
+                    multiply_chunk(q // STAGES_A_CHUNK)
+                if part == 2:
+                    store_chunk(q // STAGES_A_CHUNK)
+            if 0 <= n < STEPS and c + 1 < CHUNKS:
+                if j == 5:
+                    clamp_chunk(c + 1)
+                if j == 7:
+                    pass_chunk(c + 1)

@@ -27,14 +27,21 @@ CHUNK_ROWS = ROW_TILES * P
 CHUNKS = ROWS // CHUNK_ROWS
 PLANE = ROW_TILES * FEATURES
 STEPS = CHUNKS * KNOTS
-TURN_KNOTS = 3
-STAGES_A_CHUNK = KNOTS // TURN_KNOTS
+KNOTS_A_STAGE = 3
+STAGES_A_CHUNK = KNOTS // KNOTS_A_STAGE
 BASES_A_STAGE = BASES // STAGES_A_CHUNK
 HALVES = ((0,), (1, 2), (3,))
-LEFT_LAG = 1
-RIGHT_LAG = 2
+LEFT_LAG = 2
+RIGHT_LAG = 3
 SQUARE_AHEAD = 2
-PSUM_CHUNKS = 14
+ONE_SIDED = (
+    ("rise", 1), ("rise", 2), ("rise", 3), ("fall", 3),
+    ("rise", 4), ("fall", 4), ("rise", 5), ("fall", 5),
+    ("rise", 6), ("fall", 6), ("rise", 7), ("fall", 7),
+    ("rise", 8), ("fall", 8), ("fall", 9), ("fall", 10),
+)
+ONE_SIDED_A_STAGE = 4
+SCALAR_TAKES = tuple(u for u, side in enumerate(ONE_SIDED) if side[1] % 2 == 0 and side not in (("fall", 6), ("rise", 8)))
 
 FLOPS = 2 * ROWS * OUT_F * (FEATURES + FEATURES * BASES)
 
@@ -170,7 +177,6 @@ def tile_kanblock_pa_t_kernel(tc, x, grid, w1_base, w1_spline, out):
                 in_=weight_grouped[:, SILU_PASS, :, :].rearrange("p f t -> p (f t)"),
             )
 
-        x_second = {}
         silu = {}
         square = {}
         cube = {}
@@ -181,17 +187,6 @@ def tile_kanblock_pa_t_kernel(tc, x, grid, w1_base, w1_spline, out):
         codes = {}
         scales = {}
         acc = {}
-
-        def pass_chunk(c):
-            if c >= PSUM_CHUNKS:
-                x_second[c] = x_clamped[c]
-                return
-            x_second[c] = psum.tile([P, PLANE], BF16, name="x_psum", tag="x_psum", bufs=2)
-            for r in range(ROW_TILES):
-                cols = slice(r * FEATURES, (r + 1) * FEATURES)
-                nc.tensor.matmul(
-                    out=x_second[c][:, cols], lhsT=identity[:], rhs=x_clamped[c][:, cols], start=True, stop=True
-                )
 
         def silu_chunk(c):
             turned = psum.tile([P, PACK, CHUNK_ROWS], BF16, name="turned", tag="turned", bufs=1)
@@ -216,41 +211,36 @@ def tile_kanblock_pa_t_kernel(tc, x, grid, w1_base, w1_spline, out):
             if j == 0 or j == KNOTS - 1:
                 cube[n] = work.tile([P, PLANE], F32, name="end_cube", tag="end_cube", bufs=3)
             else:
-                cube[n] = work.tile([P, PLANE], F32, name="cube", tag="cube", bufs=4)
+                cube[n] = work.tile([P, PLANE], F32, name="cube", tag="cube", bufs=7)
             nc.vector.scalar_tensor_tensor(
                 out=cube[n][:],
-                in0=x_second[c][:],
+                in0=x_clamped[c][:],
                 scalar=knot[:, j : j + 1],
                 in1=square[n][:],
                 op0=ALU.subtract,
                 op1=ALU.mult,
             )
 
-        def one_sided_step(n):
-            j = n % KNOTS
-            if j == 0:
-                rising[n] = cube[n]
-            elif j <= BASES:
-                rising[n] = work.tile([P, PLANE], F32, name="rising", tag="rising", bufs=7)
-                nc.gpsimd.tensor_scalar(
-                    out=rising[n][:],
+        def one_sided_step(c, u):
+            kind, j = ONE_SIDED[u]
+            n = c * KNOTS + j
+            plane = work.tile([P, PLANE], F32, name=kind, tag=kind, bufs=7)
+            if kind == "rise":
+                rising[n] = plane
+                scale = rising_scale[:, j : j + 1]
+            else:
+                falling[n] = plane
+                scale = falling_scale[:, j - DEGREE : j - DEGREE + 1]
+            if u in SCALAR_TAKES:
+                nc.scalar.activation(out=plane[:], in_=cube[n][:], func=ACT.Relu, scale=scale)
+            else:
+                nc.vector.tensor_scalar(
+                    out=plane[:],
                     in0=cube[n][:],
-                    scalar1=rising_scale[:, j : j + 1],
+                    scalar1=scale,
                     scalar2=0.0,
                     op0=ALU.mult,
                     op1=ALU.max if j % 2 == 0 else ALU.min,
-                )
-            if j == KNOTS - 1:
-                falling[n] = cube[n]
-            elif j >= DEGREE:
-                falling[n] = work.tile([P, PLANE], F32, name="falling", tag="falling", bufs=7)
-                nc.gpsimd.tensor_scalar(
-                    out=falling[n][:],
-                    in0=cube[n][:],
-                    scalar1=falling_scale[:, j - DEGREE : j - DEGREE + 1],
-                    scalar2=0.0,
-                    op0=ALU.mult,
-                    op1=ALU.min if (KNOTS - 1 - j) % 2 == 0 else ALU.max,
                 )
 
         def turn_sum(tag, bufs, first, second, r):
@@ -267,13 +257,13 @@ def tile_kanblock_pa_t_kernel(tc, x, grid, w1_base, w1_spline, out):
 
         def left_branch(c, m, r):
             n = c * KNOTS + m
-            total = turn_sum("left_sum", 2, rising[n], rising[n + 1], r)
+            total = turn_sum("left_sum", 3, rising[n], rising[n + 1], r)
             left[(c, m, r)] = work.tile([P, P, PACK], BF16, name="left", tag="left", bufs=10)
             nc.scalar.activation(out=left[(c, m, r)][:], in_=total, func=ACT.Relu, scale=left_scale[:, m : m + 1])
 
         def right_branch(c, m, r):
             n = c * KNOTS + m
-            total = turn_sum("right_sum", 3, falling[n + DEGREE + 1], falling[n + DEGREE], r)
+            total = turn_sum("right_sum", 4, falling[n + DEGREE + 1], falling[n + DEGREE], r)
             group, place = divmod(m, GROUP)
             if place == 0 and r == 0:
                 basis[(c, group)] = work.tile(
@@ -328,18 +318,24 @@ def tile_kanblock_pa_t_kernel(tc, x, grid, w1_base, w1_spline, out):
             )
 
         load_weights()
-        pass_chunk(0)
         stages = CHUNKS * STAGES_A_CHUNK
-        for n in range(-SQUARE_AHEAD, (stages + 6) * TURN_KNOTS):
+        for n in range(-SQUARE_AHEAD, (stages + RIGHT_LAG + 3) * KNOTS_A_STAGE):
             c, j = divmod(n, KNOTS)
-            stage, part = divmod(n, TURN_KNOTS)
+            stage, part = divmod(n, KNOTS_A_STAGE)
             if 0 <= n < STEPS and j == 0 and c + 2 < CHUNKS:
                 load_chunk(c + 2)
             if 0 <= n + SQUARE_AHEAD < STEPS:
                 square_step(n + SQUARE_AHEAD)
             if 0 <= n < STEPS:
                 cube_step(n)
-                one_sided_step(n)
+                if j == 0:
+                    rising[n] = cube[n]
+                if j == KNOTS - 1:
+                    falling[n] = cube[n]
+            q = stage - 1
+            if 0 <= q < stages:
+                for u in HALVES[part]:
+                    one_sided_step(q // STAGES_A_CHUNK, (q % STAGES_A_CHUNK) * ONE_SIDED_A_STAGE + u)
             for half in HALVES[part]:
                 base, r = divmod(half, ROW_TILES)
                 q = stage - RIGHT_LAG
@@ -348,7 +344,7 @@ def tile_kanblock_pa_t_kernel(tc, x, grid, w1_base, w1_spline, out):
                 q = stage - LEFT_LAG
                 if 0 <= q < stages:
                     left_branch(q // STAGES_A_CHUNK, (q % STAGES_A_CHUNK) * BASES_A_STAGE + base, r)
-            if 0 <= n < STEPS and j == 1:
+            if 0 <= n < STEPS and j == 7:
                 silu_chunk(c)
             if 2 <= n < 2 + PASSES:
                 turn_weight_pass(n - 2)
@@ -366,5 +362,3 @@ def tile_kanblock_pa_t_kernel(tc, x, grid, w1_base, w1_spline, out):
             if 0 <= n < STEPS and c + 1 < CHUNKS:
                 if j == 5:
                     clamp_chunk(c + 1)
-                if j == 7:
-                    pass_chunk(c + 1)

@@ -30,18 +30,11 @@ STEPS = CHUNKS * KNOTS
 KNOTS_A_STAGE = 3
 STAGES_A_CHUNK = KNOTS // KNOTS_A_STAGE
 BASES_A_STAGE = BASES // STAGES_A_CHUNK
-HALVES = ((0,), (1, 2), (3,))
-LEFT_LAG = 2
-RIGHT_LAG = 3
+HALVES = ((0, 1), (), (2, 3))
+TAIL_LAG = 2
+BODY_LAG = 3
 SQUARE_AHEAD = 2
-ONE_SIDED = (
-    ("rise", 1), ("rise", 2), ("rise", 3), ("fall", 3),
-    ("rise", 4), ("fall", 4), ("rise", 5), ("fall", 5),
-    ("rise", 6), ("fall", 6), ("rise", 7), ("fall", 7),
-    ("rise", 8), ("fall", 8), ("fall", 9), ("fall", 10),
-)
-ONE_SIDED_A_STAGE = 4
-SCALAR_TAKES = tuple(u for u, side in enumerate(ONE_SIDED) if side[1] % 2 == 0 and side not in (("fall", 6), ("rise", 8)))
+LAST_THIRD = BASES + 1
 
 FLOPS = 2 * ROWS * OUT_F * (FEATURES + FEATURES * BASES)
 
@@ -113,38 +106,33 @@ def tile_kanblock_pa_t_kernel(tc, x, grid, w1_base, w1_spline, out):
             nc.vector.reciprocal(out=result[:], in_=result[:])
             return result
 
-        a_left = reciprocal(product("a_left", [spans(1, 0), spans(2, 0), spans(3, 0)]))
-        c_right = reciprocal(product("c_right", [spans(1, 3), spans(2, 2), spans(3, 1)]))
+        a_body = reciprocal(product("a_body", [spans(1, 0), spans(2, 0), spans(3, 0)]))
+        neg_c_tail = reciprocal(product("neg_c_tail", [spans(1, 3), spans(2, 2), spans(3, 1)]))
+        nc.vector.tensor_scalar_mul(out=neg_c_tail[:], in0=neg_c_tail[:], scalar1=-1.0)
         b_over_a = reciprocal(product("b_over_a", [spans(1, 1), spans(2, 1), spans(3, 1)]))
         b_over_a_top = product("b_over_a_top", [spans(2, 0), spans(3, 0), spans(4, 0)])
-        c_over_d = reciprocal(product("c_over_d", [spans(4, 0), spans(2, 2), spans(3, 1)]))
-        c_over_d_top = product("c_over_d_top", [spans(1, 2), spans(2, 1), spans(3, 0)])
+        w_over_a = reciprocal(product("w_over_a", [spans(1, 1), spans(1, 2), spans(2, 2)]))
+        w_over_a_top = product("w_over_a_top", [spans(1, 0), spans(3, 0), spans(4, 0)])
+        nc.vector.scalar_tensor_tensor(
+            out=b_over_a[:], in0=b_over_a[:], scalar=-1.0, in1=b_over_a_top[:], op0=ALU.mult, op1=ALU.mult
+        )
         ones = consts.tile([P, BASES], F32, name="ones")
         nc.vector.memset(ones[:], 1.0)
-
-        def running_product(name, top, below):
-            nc.vector.scalar_tensor_tensor(
-                out=below[:], in0=below[:], scalar=-1.0, in1=top[:], op0=ALU.mult, op1=ALU.mult
-            )
-            result = consts.tile([P, BASES + 1], F32, name=name)
-            nc.vector.memset(result[:, 0:1], 1.0)
-            nc.vector.tensor_tensor_scan(
-                out=result[:, 1 : BASES + 1], data0=below[:], data1=ones[:], initial=1.0, op0=ALU.mult, op1=ALU.mult
-            )
-            return result
-
-        rising_scale = running_product("rising_scale", b_over_a_top, b_over_a)
-        falling_scale = running_product("falling_scale", c_over_d_top, c_over_d)
-        last = consts.tile([P, 1], F32, name="last")
-        nc.vector.reciprocal(out=last[:], in_=falling_scale[:, BASES : BASES + 1])
-        nc.vector.tensor_scalar_mul(out=falling_scale[:], in0=falling_scale[:], scalar1=last[:])
-        left_scale = consts.tile([P, BASES], F32, name="left_scale")
-        nc.vector.reciprocal(out=left_scale[:], in_=rising_scale[:, 0:BASES])
-        nc.vector.tensor_mul(out=left_scale[:], in0=left_scale[:], in1=a_left[:])
-        right_scale = consts.tile([P, BASES], F32, name="right_scale")
-        nc.vector.reciprocal(out=right_scale[:], in_=falling_scale[:, 1 : BASES + 1])
-        nc.vector.scalar_tensor_tensor(
-            out=right_scale[:], in0=right_scale[:], scalar=-1.0, in1=c_right[:], op0=ALU.mult, op1=ALU.mult
+        first_scale = consts.tile([P, BASES + 1], F32, name="first_scale")
+        nc.vector.memset(first_scale[:, 0:1], 1.0)
+        nc.vector.tensor_tensor_scan(
+            out=first_scale[:, 1 : BASES + 1], data0=b_over_a[:], data1=ones[:], initial=1.0, op0=ALU.mult, op1=ALU.mult
+        )
+        one_over_first = consts.tile([P, BASES + 1], F32, name="one_over_first")
+        nc.vector.reciprocal(out=one_over_first[:], in_=first_scale[:])
+        body_scale = consts.tile([P, BASES], F32, name="body_scale")
+        nc.vector.tensor_mul(out=body_scale[:], in0=a_body[:], in1=one_over_first[:, 0:BASES])
+        third_scale = consts.tile([P, BASES], F32, name="third_scale")
+        nc.vector.tensor_mul(out=third_scale[:], in0=w_over_a[:], in1=w_over_a_top[:])
+        nc.vector.tensor_mul(out=third_scale[:], in0=third_scale[:], in1=first_scale[:, 0:BASES])
+        third_of_first = consts.tile([P, BASES - 1], F32, name="third_of_first")
+        nc.vector.tensor_mul(
+            out=third_of_first[:], in0=third_scale[:, 0 : BASES - 1], in1=one_over_first[:, 2 : BASES + 1]
         )
 
         spline_rows = consts.tile([P, FEATURES * BASES], BF16, name="spline_rows")
@@ -180,9 +168,9 @@ def tile_kanblock_pa_t_kernel(tc, x, grid, w1_base, w1_spline, out):
         silu = {}
         square = {}
         cube = {}
-        rising = {}
-        falling = {}
-        left = {}
+        first = {}
+        third = {}
+        tail = {}
         basis = {}
         codes = {}
         scales = {}
@@ -208,10 +196,11 @@ def tile_kanblock_pa_t_kernel(tc, x, grid, w1_base, w1_spline, out):
 
         def cube_step(n):
             c, j = divmod(n, KNOTS)
-            if j == 0 or j == KNOTS - 1:
-                cube[n] = work.tile([P, PLANE], F32, name="end_cube", tag="end_cube", bufs=3)
+            if j == 0:
+                cube[n] = work.tile([P, PLANE], F32, name="first_cube", tag="first_cube", bufs=2)
+                first[n] = cube[n]
             else:
-                cube[n] = work.tile([P, PLANE], F32, name="cube", tag="cube", bufs=7)
+                cube[n] = work.tile([P, PLANE], F32, name="cube", tag="cube", bufs=8)
             nc.vector.scalar_tensor_tensor(
                 out=cube[n][:],
                 in0=x_clamped[c][:],
@@ -221,49 +210,54 @@ def tile_kanblock_pa_t_kernel(tc, x, grid, w1_base, w1_spline, out):
                 op1=ALU.mult,
             )
 
-        def one_sided_step(c, u):
-            kind, j = ONE_SIDED[u]
-            n = c * KNOTS + j
-            plane = work.tile([P, PLANE], F32, name=kind, tag=kind, bufs=7)
-            if kind == "rise":
-                rising[n] = plane
-                scale = rising_scale[:, j : j + 1]
-            else:
-                falling[n] = plane
-                scale = falling_scale[:, j - DEGREE : j - DEGREE + 1]
-            if u in SCALAR_TAKES:
+        def one_sided_step(n):
+            j = n % KNOTS
+            plane = work.tile([P, PLANE], F32, name="first", tag="first", bufs=10)
+            scale = third_scale[:, BASES - 1 : BASES] if j == LAST_THIRD else first_scale[:, j : j + 1]
+            if j % 2 == 0:
                 nc.scalar.activation(out=plane[:], in_=cube[n][:], func=ACT.Relu, scale=scale)
             else:
                 nc.vector.tensor_scalar(
-                    out=plane[:],
-                    in0=cube[n][:],
-                    scalar1=scale,
+                    out=plane[:], in0=cube[n][:], scalar1=scale, scalar2=0.0, op0=ALU.mult, op1=ALU.min
+                )
+            if j == LAST_THIRD:
+                third[n] = plane
+                return
+            first[n] = plane
+            if j >= 2:
+                third[n] = work.tile([P, PLANE], F32, name="third", tag="third", bufs=8)
+                nc.gpsimd.tensor_scalar(
+                    out=third[n][:],
+                    in0=plane[:],
+                    scalar1=third_of_first[:, j - 2 : j - 1],
                     scalar2=0.0,
                     op0=ALU.mult,
-                    op1=ALU.max if j % 2 == 0 else ALU.min,
+                    op1=ALU.add,
                 )
 
-        def turn_sum(tag, bufs, first, second, r):
+        def turn_sum(tag, bufs, planes, r):
             total = psum.tile([P, PACK, P], F32, name=tag, tag=tag, bufs=bufs)
             for t in range(PACK):
                 cols = slice(r * FEATURES + t * P, r * FEATURES + (t + 1) * P)
-                nc.tensor.matmul(
-                    out=total[:, t, :], lhsT=first[:, cols], rhs=identity_f32[:], is_transpose=True, start=True, stop=False
-                )
-                nc.tensor.matmul(
-                    out=total[:, t, :], lhsT=second[:, cols], rhs=identity_f32[:], is_transpose=True, start=False, stop=True
-                )
+                for i, plane in enumerate(planes):
+                    nc.tensor.matmul(
+                        out=total[:, t, :],
+                        lhsT=plane[:, cols],
+                        rhs=identity_f32[:],
+                        is_transpose=True,
+                        start=(i == 0),
+                        stop=(i == len(planes) - 1),
+                    )
             return total[:].rearrange("p t n -> p n t")
 
-        def left_branch(c, m, r):
-            n = c * KNOTS + m
-            total = turn_sum("left_sum", 3, rising[n], rising[n + 1], r)
-            left[(c, m, r)] = work.tile([P, P, PACK], BF16, name="left", tag="left", bufs=10)
-            nc.scalar.activation(out=left[(c, m, r)][:], in_=total, func=ACT.Relu, scale=left_scale[:, m : m + 1])
+        def tail_step(c, m, r):
+            turned = turn_sum("tail_turned", 3, [cube[c * KNOTS + m + DEGREE + 1]], r)
+            tail[(c, m, r)] = work.tile([P, P, PACK], BF16, name="tail", tag="tail", bufs=10)
+            nc.scalar.activation(out=tail[(c, m, r)][:], in_=turned, func=ACT.Relu, scale=neg_c_tail[:, m : m + 1])
 
-        def right_branch(c, m, r):
+        def body_step(c, m, r):
             n = c * KNOTS + m
-            total = turn_sum("right_sum", 4, falling[n + DEGREE + 1], falling[n + DEGREE], r)
+            total = turn_sum("body_sum", 4, [first[n], first[n + 1], third[n + 2]], r)
             group, place = divmod(m, GROUP)
             if place == 0 and r == 0:
                 basis[(c, group)] = work.tile(
@@ -272,10 +266,10 @@ def tile_kanblock_pa_t_kernel(tc, x, grid, w1_base, w1_spline, out):
             nc.vector.scalar_tensor_tensor(
                 out=basis[(c, group)][:, place, r * P : (r + 1) * P, :],
                 in0=total,
-                scalar=right_scale[:, m : m + 1],
-                in1=left[(c, m, r)][:],
+                scalar=body_scale[:, m : m + 1],
+                in1=tail[(c, m, r)][:],
                 op0=ALU.mult,
-                op1=ALU.max,
+                op1=ALU.min,
             )
 
         def quantise_group(c, group):
@@ -319,7 +313,7 @@ def tile_kanblock_pa_t_kernel(tc, x, grid, w1_base, w1_spline, out):
 
         load_weights()
         stages = CHUNKS * STAGES_A_CHUNK
-        for n in range(-SQUARE_AHEAD, (stages + RIGHT_LAG + 3) * KNOTS_A_STAGE):
+        for n in range(-SQUARE_AHEAD, (stages + BODY_LAG + 3) * KNOTS_A_STAGE):
             c, j = divmod(n, KNOTS)
             stage, part = divmod(n, KNOTS_A_STAGE)
             if 0 <= n < STEPS and j == 0 and c + 2 < CHUNKS:
@@ -328,32 +322,26 @@ def tile_kanblock_pa_t_kernel(tc, x, grid, w1_base, w1_spline, out):
                 square_step(n + SQUARE_AHEAD)
             if 0 <= n < STEPS:
                 cube_step(n)
-                if j == 0:
-                    rising[n] = cube[n]
-                if j == KNOTS - 1:
-                    falling[n] = cube[n]
-            q = stage - 1
-            if 0 <= q < stages:
-                for u in HALVES[part]:
-                    one_sided_step(q // STAGES_A_CHUNK, (q % STAGES_A_CHUNK) * ONE_SIDED_A_STAGE + u)
+            if 0 <= n - 1 < STEPS and 1 <= (n - 1) % KNOTS <= LAST_THIRD:
+                one_sided_step(n - 1)
             for half in HALVES[part]:
                 base, r = divmod(half, ROW_TILES)
-                q = stage - RIGHT_LAG
+                q = stage - BODY_LAG
                 if 0 <= q < stages:
-                    right_branch(q // STAGES_A_CHUNK, (q % STAGES_A_CHUNK) * BASES_A_STAGE + base, r)
-                q = stage - LEFT_LAG
+                    body_step(q // STAGES_A_CHUNK, (q % STAGES_A_CHUNK) * BASES_A_STAGE + base, r)
+                q = stage - TAIL_LAG
                 if 0 <= q < stages:
-                    left_branch(q // STAGES_A_CHUNK, (q % STAGES_A_CHUNK) * BASES_A_STAGE + base, r)
+                    tail_step(q // STAGES_A_CHUNK, (q % STAGES_A_CHUNK) * BASES_A_STAGE + base, r)
             if 0 <= n < STEPS and j == 7:
                 silu_chunk(c)
             if 2 <= n < 2 + PASSES:
                 turn_weight_pass(n - 2)
             if n == KNOTS:
                 quantise_weights()
-            q = stage - RIGHT_LAG - 1
+            q = stage - BODY_LAG - 1
             if part == 1 and 0 <= q < stages and q % 2 == 1:
                 quantise_group(q // STAGES_A_CHUNK, (q % STAGES_A_CHUNK) // 2)
-            q = stage - RIGHT_LAG - 2
+            q = stage - BODY_LAG - 2
             if 0 <= q < stages and q % STAGES_A_CHUNK == STAGES_A_CHUNK - 1:
                 if part == 0:
                     multiply_chunk(q // STAGES_A_CHUNK)

@@ -22,10 +22,10 @@ BASES = KNOTS - DEGREE - 1
 PASSES = BASES + 1
 SILU_PASS = BASES
 GROUP = 4
-ROW_TILES = 2
-CHUNK_ROWS = ROW_TILES * P
-CHUNKS = ROWS // CHUNK_ROWS
-PLANE = ROW_TILES * FEATURES
+MOST_ROW_TILES = 2
+ROW_TILES = (MOST_ROW_TILES,) * 15 + (1, 1)
+CHUNKS = len(ROW_TILES)
+FIRST_ROW = tuple(P * sum(ROW_TILES[:c]) for c in range(CHUNKS))
 STEPS = CHUNKS * KNOTS
 KNOTS_A_STAGE = 3
 STAGES_A_CHUNK = KNOTS // KNOTS_A_STAGE
@@ -34,6 +34,7 @@ HALVES = ((0, 1), (), (2, 3))
 TAIL_LAG = 2
 BODY_LAG = 3
 SQUARE_AHEAD = 2
+SCALAR_KNOTS = (2, 4, 6, 8)
 LAST_THIRD = BASES + 1
 
 FLOPS = 2 * ROWS * OUT_F * (FEATURES + FEATURES * BASES)
@@ -54,13 +55,18 @@ def tile_kanblock_pa_t_kernel(tc, x, grid, w1_base, w1_spline, out):
         identity_f32 = consts.tile([P, P], F32, name="identity_f32")
         make_identity(nc, identity_f32[:])
 
+        def rows_of(c):
+            return slice(FIRST_ROW[c], FIRST_ROW[c] + P * ROW_TILES[c])
+
+        def plane_tile(c, dtype, tag, bufs):
+            return work.tile([P, ROW_TILES[c] * FEATURES], dtype, name=tag, tag=tag, bufs=bufs)
+
         x_rows = {}
 
         def load_chunk(c):
-            x_rows[c] = work.tile([P, PLANE], BF16, name="x_rows", tag="x_rows", bufs=3)
+            x_rows[c] = plane_tile(c, BF16, "x_rows", 3)
             nc.sync.dma_start(
-                out=x_rows[c][:],
-                in_=xf[c * CHUNK_ROWS : (c + 1) * CHUNK_ROWS, :].rearrange("(p r) i -> p (r i)", r=ROW_TILES),
+                out=x_rows[c][:], in_=xf[rows_of(c), :].rearrange("(p r) i -> p (r i)", r=ROW_TILES[c])
             )
 
         knot_bf = consts.tile([P, KNOTS], BF16, name="knot_bf")
@@ -75,7 +81,7 @@ def tile_kanblock_pa_t_kernel(tc, x, grid, w1_base, w1_spline, out):
         x_clamped = {}
 
         def clamp_chunk(c):
-            x_clamped[c] = work.tile([P, PLANE], BF16, name="x_clamped", tag="x_clamped", bufs=3)
+            x_clamped[c] = plane_tile(c, BF16, "x_clamped", 3)
             nc.vector.tensor_scalar(
                 out=x_clamped[c][:],
                 in0=x_rows[c][:],
@@ -151,7 +157,7 @@ def tile_kanblock_pa_t_kernel(tc, x, grid, w1_base, w1_spline, out):
             turned = psum.tile([P, PACK, P], BF16, name="turned", tag="turned", bufs=1)
             for t in range(PACK):
                 nc.tensor.transpose(turned[:, t, :], rows[:, t * P : (t + 1) * P], identity[:])
-            nc.scalar.copy(out=weight_grouped[:, k, :, :], in_=turned[:].rearrange("p t r -> p r t"))
+            nc.vector.tensor_copy(out=weight_grouped[:, k, :, :], in_=turned[:].rearrange("p t r -> p r t"))
 
         def quantise_weights():
             nc.vector.quantize_mx(
@@ -177,19 +183,19 @@ def tile_kanblock_pa_t_kernel(tc, x, grid, w1_base, w1_spline, out):
         acc = {}
 
         def silu_chunk(c):
-            turned = psum.tile([P, PACK, CHUNK_ROWS], BF16, name="turned", tag="turned", bufs=1)
-            for r in range(ROW_TILES):
+            turned = psum.tile([P, PACK, P * ROW_TILES[c]], BF16, name="turned", tag="turned", bufs=1)
+            for r in range(ROW_TILES[c]):
                 for t in range(PACK):
                     first = r * FEATURES + t * P
                     nc.tensor.transpose(
                         turned[:, t, r * P : (r + 1) * P], x_rows[c][:, first : first + P], identity[:]
                     )
-            silu[c] = work.tile([P, CHUNK_ROWS, PACK], BF16, name="silu", tag="silu", align_bytes=64)
+            silu[c] = work.tile([P, P * ROW_TILES[c], PACK], BF16, name="silu", tag="silu", align_bytes=64)
             nc.scalar.activation(out=silu[c][:], in_=turned[:].rearrange("p t n -> p n t"), func=ACT.Silu)
 
         def square_step(n):
             c, j = divmod(n, KNOTS)
-            square[n] = work.tile([P, PLANE], F32, name="square", tag="square", bufs=SQUARE_AHEAD + 2)
+            square[n] = plane_tile(c, F32, "square", SQUARE_AHEAD + 2)
             nc.scalar.activation(
                 out=square[n][:], in_=x_clamped[c][:], func=ACT.Square, bias=neg_knot[:, j : j + 1], scale=1.0
             )
@@ -197,10 +203,10 @@ def tile_kanblock_pa_t_kernel(tc, x, grid, w1_base, w1_spline, out):
         def cube_step(n):
             c, j = divmod(n, KNOTS)
             if j == 0:
-                cube[n] = work.tile([P, PLANE], F32, name="first_cube", tag="first_cube", bufs=2)
+                cube[n] = plane_tile(c, F32, "first_cube", 2)
                 first[n] = cube[n]
             else:
-                cube[n] = work.tile([P, PLANE], F32, name="cube", tag="cube", bufs=8)
+                cube[n] = plane_tile(c, F32, "cube", 8)
             nc.vector.scalar_tensor_tensor(
                 out=cube[n][:],
                 in0=x_clamped[c][:],
@@ -211,21 +217,26 @@ def tile_kanblock_pa_t_kernel(tc, x, grid, w1_base, w1_spline, out):
             )
 
         def one_sided_step(n):
-            j = n % KNOTS
-            plane = work.tile([P, PLANE], F32, name="first", tag="first", bufs=10)
+            c, j = divmod(n, KNOTS)
+            plane = plane_tile(c, F32, "first", 10)
             scale = third_scale[:, BASES - 1 : BASES] if j == LAST_THIRD else first_scale[:, j : j + 1]
-            if j % 2 == 0:
+            if j in SCALAR_KNOTS and n >= KNOTS:
                 nc.scalar.activation(out=plane[:], in_=cube[n][:], func=ACT.Relu, scale=scale)
             else:
                 nc.vector.tensor_scalar(
-                    out=plane[:], in0=cube[n][:], scalar1=scale, scalar2=0.0, op0=ALU.mult, op1=ALU.min
+                    out=plane[:],
+                    in0=cube[n][:],
+                    scalar1=scale,
+                    scalar2=0.0,
+                    op0=ALU.mult,
+                    op1=ALU.max if j % 2 == 0 else ALU.min,
                 )
             if j == LAST_THIRD:
                 third[n] = plane
                 return
             first[n] = plane
             if j >= 2:
-                third[n] = work.tile([P, PLANE], F32, name="third", tag="third", bufs=8)
+                third[n] = plane_tile(c, F32, "third", 8)
                 nc.gpsimd.tensor_scalar(
                     out=third[n][:],
                     in0=plane[:],
@@ -237,16 +248,15 @@ def tile_kanblock_pa_t_kernel(tc, x, grid, w1_base, w1_spline, out):
 
         def turn_sum(tag, bufs, planes, r):
             total = psum.tile([P, PACK, P], F32, name=tag, tag=tag, bufs=bufs)
-            for t in range(PACK):
-                cols = slice(r * FEATURES + t * P, r * FEATURES + (t + 1) * P)
-                for i, plane in enumerate(planes):
+            for i, plane in enumerate(planes):
+                for t in range(PACK):
                     nc.tensor.matmul(
                         out=total[:, t, :],
-                        lhsT=plane[:, cols],
+                        lhsT=plane[:, r * FEATURES + t * P : r * FEATURES + (t + 1) * P],
                         rhs=identity_f32[:],
                         is_transpose=True,
-                        start=(i == 0),
-                        stop=(i == len(planes) - 1),
+                        start=(i == 0 and t == 0),
+                        stop=(i == len(planes) - 1 and t == PACK - 1),
                     )
             return total[:].rearrange("p t n -> p n t")
 
@@ -261,7 +271,7 @@ def tile_kanblock_pa_t_kernel(tc, x, grid, w1_base, w1_spline, out):
             group, place = divmod(m, GROUP)
             if place == 0 and r == 0:
                 basis[(c, group)] = work.tile(
-                    [P, GROUP, CHUNK_ROWS, PACK], BF16, name="basis", tag="basis", bufs=3, align_bytes=64
+                    [P, GROUP, P * ROW_TILES[c], PACK], BF16, name="basis", tag="basis", bufs=3, align_bytes=64
                 )
             nc.vector.scalar_tensor_tensor(
                 out=basis[(c, group)][:, place, r * P : (r + 1) * P, :],
@@ -274,8 +284,9 @@ def tile_kanblock_pa_t_kernel(tc, x, grid, w1_base, w1_spline, out):
 
         def quantise_group(c, group):
             if group == 0:
-                codes[c] = work.tile([P, PASSES, CHUNK_ROWS], U32, name="codes", tag="codes", align_bytes=64)
-                scales[c] = work.tile([P, PASSES, CHUNK_ROWS], U8, name="scales", tag="scales", align_bytes=64)
+                shape = [P, PASSES, P * ROW_TILES[c]]
+                codes[c] = work.tile(shape, U32, name="codes", tag="codes", align_bytes=64)
+                scales[c] = work.tile(shape, U8, name="scales", tag="scales", align_bytes=64)
                 nc.vector.quantize_mx(
                     out=codes[c][:, SILU_PASS, :].bitcast(FP8X4),
                     scales=scales[c][:, SILU_PASS, :],
@@ -289,8 +300,8 @@ def tile_kanblock_pa_t_kernel(tc, x, grid, w1_base, w1_spline, out):
             )
 
         def multiply_chunk(c):
-            acc[c] = psum.tile([P, ROW_TILES, OUT_F], F32, name="acc", tag="turned", bufs=1)
-            for r in range(ROW_TILES):
+            acc[c] = psum.tile([P, ROW_TILES[c], OUT_F], F32, name="acc", tag="turned", bufs=1)
+            for r in range(ROW_TILES[c]):
                 row_cols = slice(r * P, (r + 1) * P)
                 for k in range(PASSES):
                     nc.tensor.matmul_mx(
@@ -304,10 +315,10 @@ def tile_kanblock_pa_t_kernel(tc, x, grid, w1_base, w1_spline, out):
                     )
 
         def store_chunk(c):
-            out_rows = work.tile([P, ROW_TILES, OUT_F], F32, name="out_rows", tag="out_rows")
+            out_rows = work.tile([P, ROW_TILES[c], OUT_F], F32, name="out_rows", tag="out_rows")
             nc.scalar.copy(out=out_rows[:], in_=acc[c][:])
             nc.sync.dma_start(
-                out=out[c * CHUNK_ROWS : (c + 1) * CHUNK_ROWS, :].rearrange("(p r) f -> p r f", r=ROW_TILES),
+                out=out[rows_of(c), :].rearrange("(p r) f -> p r f", r=ROW_TILES[c]),
                 in_=out_rows[:],
             )
 
@@ -325,13 +336,11 @@ def tile_kanblock_pa_t_kernel(tc, x, grid, w1_base, w1_spline, out):
             if 0 <= n - 1 < STEPS and 1 <= (n - 1) % KNOTS <= LAST_THIRD:
                 one_sided_step(n - 1)
             for half in HALVES[part]:
-                base, r = divmod(half, ROW_TILES)
-                q = stage - BODY_LAG
-                if 0 <= q < stages:
-                    body_step(q // STAGES_A_CHUNK, (q % STAGES_A_CHUNK) * BASES_A_STAGE + base, r)
-                q = stage - TAIL_LAG
-                if 0 <= q < stages:
-                    tail_step(q // STAGES_A_CHUNK, (q % STAGES_A_CHUNK) * BASES_A_STAGE + base, r)
+                base, r = divmod(half, MOST_ROW_TILES)
+                for lag, step in ((BODY_LAG, body_step), (TAIL_LAG, tail_step)):
+                    chunk, q = divmod(stage - lag, STAGES_A_CHUNK)
+                    if 0 <= chunk < CHUNKS and r < ROW_TILES[chunk]:
+                        step(chunk, q * BASES_A_STAGE + base, r)
             if 0 <= n < STEPS and j == 7:
                 silu_chunk(c)
             if 2 <= n < 2 + PASSES:

from contextlib import ExitStack

import concourse.mybir as mybir
from concourse.masks import make_identity

F32 = mybir.dt.float32
BF16 = mybir.dt.bfloat16
U32 = mybir.dt.uint32
U8 = mybir.dt.uint8
FP8X4 = mybir.dt.float8_e4m3fn_x4
ACT = mybir.ActivationFunctionType
ALU = mybir.AluOpType

P = 128
PACK = 4
ROWS = 4096
FEATURES = P * PACK
OUT_F = 128
DEGREE = 3
KNOTS = 12
BASES = KNOTS - DEGREE - 1
PASSES = BASES + 1
SILU_PASS = BASES
GROUP = 4
MOST_ROW_TILES = 2
ROW_TILES = (MOST_ROW_TILES,) * 15 + (1, 1)
CHUNKS = len(ROW_TILES)
FIRST_ROW = tuple(P * sum(ROW_TILES[:c]) for c in range(CHUNKS))
STEPS = CHUNKS * KNOTS
KNOTS_A_STAGE = 3
STAGES_A_CHUNK = KNOTS // KNOTS_A_STAGE
BASES_A_STAGE = BASES // STAGES_A_CHUNK
HALVES = ((0, 1), (), (2, 3))
TAIL_LAG = 2
BODY_LAG = 3
SQUARE_AHEAD = 2
SCALAR_KNOTS = (2, 4, 6, 8)
LAST_THIRD = BASES + 1

FLOPS = 2 * ROWS * OUT_F * (FEATURES + FEATURES * BASES)


def tile_kanblock_pa_t_kernel(tc, x, grid, w1_base, w1_spline, out):
    nc = tc.nc
    xf = x.flatten_outer_dims()

    with ExitStack() as ctx:
        ctx.enter_context(tc.manual_schedule())
        consts = ctx.enter_context(tc.tile_pool(name="consts", bufs=1))
        work = ctx.enter_context(tc.tile_pool(name="work", bufs=2))
        psum = ctx.enter_context(tc.psum_pool(name="psum", bufs=2))

        identity = consts.tile([P, P], BF16, name="identity")
        make_identity(nc, identity[:])
        identity_f32 = consts.tile([P, P], F32, name="identity_f32")
        make_identity(nc, identity_f32[:])

        def rows_of(c):
            return slice(FIRST_ROW[c], FIRST_ROW[c] + P * ROW_TILES[c])

        def plane_tile(c, dtype, tag, bufs):
            return work.tile([P, ROW_TILES[c] * FEATURES], dtype, name=tag, tag=tag, bufs=bufs)

        x_rows = {}

        def load_chunk(c):
            x_rows[c] = plane_tile(c, BF16, "x_rows", 3)
            nc.sync.dma_start(
                out=x_rows[c][:], in_=xf[rows_of(c), :].rearrange("(p r) i -> p (r i)", r=ROW_TILES[c])
            )

        knot_bf = consts.tile([P, KNOTS], BF16, name="knot_bf")
        nc.sync.dma_start(out=knot_bf[:], in_=grid.partition_broadcast(P))
        load_chunk(0)
        load_chunk(1)
        knot = consts.tile([P, KNOTS], F32, name="knot")
        nc.vector.tensor_copy(out=knot[:], in_=knot_bf[:])
        neg_knot = consts.tile([P, KNOTS], F32, name="neg_knot")
        nc.vector.tensor_scalar_mul(out=neg_knot[:], in0=knot[:], scalar1=-1.0)

        x_clamped = {}

        def clamp_chunk(c):
            x_clamped[c] = plane_tile(c, BF16, "x_clamped", 3)
            nc.vector.tensor_scalar(
                out=x_clamped[c][:],
                in0=x_rows[c][:],
                scalar1=knot[:, 0:1],
                scalar2=knot[:, KNOTS - 1 : KNOTS],
                op0=ALU.max,
                op1=ALU.min,
            )

        clamp_chunk(0)

        span = {}
        for k in range(1, DEGREE + 2):
            span[k] = consts.tile([P, KNOTS - k], F32, name="span%d" % k)
            nc.vector.tensor_sub(out=span[k][:], in0=knot[:, k:KNOTS], in1=knot[:, 0 : KNOTS - k])

        def spans(k, first):
            return span[k][:, first : first + BASES]

        def product(name, factors):
            result = consts.tile([P, BASES], F32, name=name)
            nc.vector.tensor_mul(out=result[:], in0=factors[0], in1=factors[1])
            for factor in factors[2:]:
                nc.vector.tensor_mul(out=result[:], in0=result[:], in1=factor)
            return result

        def reciprocal(result):
            nc.vector.reciprocal(out=result[:], in_=result[:])
            return result

        a_body = reciprocal(product("a_body", [spans(1, 0), spans(2, 0), spans(3, 0)]))
        neg_c_tail = reciprocal(product("neg_c_tail", [spans(1, 3), spans(2, 2), spans(3, 1)]))
        nc.vector.tensor_scalar_mul(out=neg_c_tail[:], in0=neg_c_tail[:], scalar1=-1.0)
        b_over_a = reciprocal(product("b_over_a", [spans(1, 1), spans(2, 1), spans(3, 1)]))
        b_over_a_top = product("b_over_a_top", [spans(2, 0), spans(3, 0), spans(4, 0)])
        w_over_a = reciprocal(product("w_over_a", [spans(1, 1), spans(1, 2), spans(2, 2)]))
        w_over_a_top = product("w_over_a_top", [spans(1, 0), spans(3, 0), spans(4, 0)])
        nc.vector.scalar_tensor_tensor(
            out=b_over_a[:], in0=b_over_a[:], scalar=-1.0, in1=b_over_a_top[:], op0=ALU.mult, op1=ALU.mult
        )
        ones = consts.tile([P, BASES], F32, name="ones")
        nc.vector.memset(ones[:], 1.0)
        first_scale = consts.tile([P, BASES + 1], F32, name="first_scale")
        nc.vector.memset(first_scale[:, 0:1], 1.0)
        nc.vector.tensor_tensor_scan(
            out=first_scale[:, 1 : BASES + 1], data0=b_over_a[:], data1=ones[:], initial=1.0, op0=ALU.mult, op1=ALU.mult
        )
        one_over_first = consts.tile([P, BASES + 1], F32, name="one_over_first")
        nc.vector.reciprocal(out=one_over_first[:], in_=first_scale[:])
        body_scale = consts.tile([P, BASES], F32, name="body_scale")
        nc.vector.tensor_mul(out=body_scale[:], in0=a_body[:], in1=one_over_first[:, 0:BASES])
        third_scale = consts.tile([P, BASES], F32, name="third_scale")
        nc.vector.tensor_mul(out=third_scale[:], in0=w_over_a[:], in1=w_over_a_top[:])
        nc.vector.tensor_mul(out=third_scale[:], in0=third_scale[:], in1=first_scale[:, 0:BASES])
        third_of_first = consts.tile([P, BASES - 1], F32, name="third_of_first")
        nc.vector.tensor_mul(
            out=third_of_first[:], in0=third_scale[:, 0 : BASES - 1], in1=one_over_first[:, 2 : BASES + 1]
        )

        spline_rows = consts.tile([P, FEATURES * BASES], BF16, name="spline_rows")
        spline_by_basis = spline_rows[:].rearrange("f (i g) -> f g i", g=BASES)
        base_rows = consts.tile([P, FEATURES], BF16, name="base_rows")
        weight_grouped = consts.tile([P, PASSES, OUT_F, PACK], BF16, name="weight_grouped", align_bytes=64)
        weight_codes = consts.tile([P, PASSES, OUT_F], U32, name="weight_codes", align_bytes=64)
        weight_scales = consts.tile([P, PASSES, OUT_F], U8, name="weight_scales", align_bytes=64)

        def load_weights():
            nc.sync.dma_start(out=spline_rows[:], in_=w1_spline.rearrange("f i g -> f (i g)"))
            nc.sync.dma_start(out=base_rows[:], in_=w1_base)

        def turn_weight_pass(k):
            rows = base_rows[:] if k == SILU_PASS else spline_by_basis[:, k, :]
            turned = psum.tile([P, PACK, P], BF16, name="turned", tag="turned", bufs=1)
            for t in range(PACK):
                nc.tensor.transpose(turned[:, t, :], rows[:, t * P : (t + 1) * P], identity[:])
            nc.vector.tensor_copy(out=weight_grouped[:, k, :, :], in_=turned[:].rearrange("p t r -> p r t"))

        def quantise_weights():
            nc.vector.quantize_mx(
                out=weight_codes[:, 0:BASES, :].rearrange("p k f -> p (k f)").bitcast(FP8X4),
                scales=weight_scales[:, 0:BASES, :].rearrange("p k f -> p (k f)"),
                in_=weight_grouped[:, 0:BASES, :, :].rearrange("p k f t -> p (k f t)"),
            )
            nc.vector.quantize_mx(
                out=weight_codes[:, SILU_PASS, :].bitcast(FP8X4),
                scales=weight_scales[:, SILU_PASS, :],
                in_=weight_grouped[:, SILU_PASS, :, :].rearrange("p f t -> p (f t)"),
            )

        silu = {}
        square = {}
        cube = {}
        first = {}
        third = {}
        tail = {}
        basis = {}
        codes = {}
        scales = {}
        acc = {}

        def silu_chunk(c):
            turned = psum.tile([P, PACK, P * ROW_TILES[c]], BF16, name="turned", tag="turned", bufs=1)
            for r in range(ROW_TILES[c]):
                for t in range(PACK):
                    first = r * FEATURES + t * P
                    nc.tensor.transpose(
                        turned[:, t, r * P : (r + 1) * P], x_rows[c][:, first : first + P], identity[:]
                    )
            silu[c] = work.tile([P, P * ROW_TILES[c], PACK], BF16, name="silu", tag="silu", align_bytes=64)
            nc.scalar.activation(out=silu[c][:], in_=turned[:].rearrange("p t n -> p n t"), func=ACT.Silu)

        def square_step(n):
            c, j = divmod(n, KNOTS)
            square[n] = plane_tile(c, F32, "square", SQUARE_AHEAD + 2)
            nc.scalar.activation(
                out=square[n][:], in_=x_clamped[c][:], func=ACT.Square, bias=neg_knot[:, j : j + 1], scale=1.0
            )

        def cube_step(n):
            c, j = divmod(n, KNOTS)
            if j == 0:
                cube[n] = plane_tile(c, F32, "first_cube", 2)
                first[n] = cube[n]
            else:
                cube[n] = plane_tile(c, F32, "cube", 8)
            nc.vector.scalar_tensor_tensor(
                out=cube[n][:],
                in0=x_clamped[c][:],
                scalar=knot[:, j : j + 1],
                in1=square[n][:],
                op0=ALU.subtract,
                op1=ALU.mult,
            )

        def one_sided_step(n):
            c, j = divmod(n, KNOTS)
            plane = plane_tile(c, F32, "first", 10)
            scale = third_scale[:, BASES - 1 : BASES] if j == LAST_THIRD else first_scale[:, j : j + 1]
            if j in SCALAR_KNOTS and n >= KNOTS:
                nc.scalar.activation(out=plane[:], in_=cube[n][:], func=ACT.Relu, scale=scale)
            else:
                nc.vector.tensor_scalar(
                    out=plane[:],
                    in0=cube[n][:],
                    scalar1=scale,
                    scalar2=0.0,
                    op0=ALU.mult,
                    op1=ALU.max if j % 2 == 0 else ALU.min,
                )
            if j == LAST_THIRD:
                third[n] = plane
                return
            first[n] = plane
            if j >= 2:
                third[n] = plane_tile(c, F32, "third", 8)
                nc.gpsimd.tensor_scalar(
                    out=third[n][:],
                    in0=plane[:],
                    scalar1=third_of_first[:, j - 2 : j - 1],
                    scalar2=0.0,
                    op0=ALU.mult,
                    op1=ALU.add,
                )

        def turn_sum(tag, bufs, planes, r):
            total = psum.tile([P, PACK, P], F32, name=tag, tag=tag, bufs=bufs)
            for i, plane in enumerate(planes):
                for t in range(PACK):
                    nc.tensor.matmul(
                        out=total[:, t, :],
                        lhsT=plane[:, r * FEATURES + t * P : r * FEATURES + (t + 1) * P],
                        rhs=identity_f32[:],
                        is_transpose=True,
                        start=(i == 0 and t == 0),
                        stop=(i == len(planes) - 1 and t == PACK - 1),
                    )
            return total[:].rearrange("p t n -> p n t")

        def tail_step(c, m, r):
            turned = turn_sum("tail_turned", 3, [cube[c * KNOTS + m + DEGREE + 1]], r)
            tail[(c, m, r)] = work.tile([P, P, PACK], BF16, name="tail", tag="tail", bufs=10)
            nc.scalar.activation(out=tail[(c, m, r)][:], in_=turned, func=ACT.Relu, scale=neg_c_tail[:, m : m + 1])

        def body_step(c, m, r):
            n = c * KNOTS + m
            total = turn_sum("body_sum", 4, [first[n], first[n + 1], third[n + 2]], r)
            group, place = divmod(m, GROUP)
            if place == 0 and r == 0:
                basis[(c, group)] = work.tile(
                    [P, GROUP, P * ROW_TILES[c], PACK], BF16, name="basis", tag="basis", bufs=3, align_bytes=64
                )
            nc.vector.scalar_tensor_tensor(
                out=basis[(c, group)][:, place, r * P : (r + 1) * P, :],
                in0=total,
                scalar=body_scale[:, m : m + 1],
                in1=tail[(c, m, r)][:],
                op0=ALU.mult,
                op1=ALU.min,
            )

        def quantise_group(c, group):
            if group == 0:
                shape = [P, PASSES, P * ROW_TILES[c]]
                codes[c] = work.tile(shape, U32, name="codes", tag="codes", align_bytes=64)
                scales[c] = work.tile(shape, U8, name="scales", tag="scales", align_bytes=64)
                nc.vector.quantize_mx(
                    out=codes[c][:, SILU_PASS, :].bitcast(FP8X4),
                    scales=scales[c][:, SILU_PASS, :],
                    in_=silu[c][:].rearrange("p n t -> p (n t)"),
                )
            planes = slice(group * GROUP, (group + 1) * GROUP)
            nc.vector.quantize_mx(
                out=codes[c][:, planes, :].rearrange("p k n -> p (k n)").bitcast(FP8X4),
                scales=scales[c][:, planes, :].rearrange("p k n -> p (k n)"),
                in_=basis[(c, group)][:].rearrange("p k n t -> p (k n t)"),
            )

        def multiply_chunk(c):
            acc[c] = psum.tile([P, ROW_TILES[c], OUT_F], F32, name="acc", tag="turned", bufs=1)
            for r in range(ROW_TILES[c]):
                row_cols = slice(r * P, (r + 1) * P)
                for k in range(PASSES):
                    nc.tensor.matmul_mx(
                        out=acc[c][:, r, :],
                        lhsT=codes[c][:, k, row_cols].bitcast(FP8X4),
                        lhsT_scale=scales[c][:, k, row_cols],
                        rhs=weight_codes[:, k, :].bitcast(FP8X4),
                        rhs_scale=weight_scales[:, k, :],
                        start=(k == 0),
                        stop=(k == PASSES - 1),
                    )

        def store_chunk(c):
            out_rows = work.tile([P, ROW_TILES[c], OUT_F], F32, name="out_rows", tag="out_rows")
            nc.scalar.copy(out=out_rows[:], in_=acc[c][:])
            nc.sync.dma_start(
                out=out[rows_of(c), :].rearrange("(p r) f -> p r f", r=ROW_TILES[c]),
                in_=out_rows[:],
            )

        load_weights()
        stages = CHUNKS * STAGES_A_CHUNK
        for n in range(-SQUARE_AHEAD, (stages + BODY_LAG + 3) * KNOTS_A_STAGE):
            c, j = divmod(n, KNOTS)
            stage, part = divmod(n, KNOTS_A_STAGE)
            if 0 <= n < STEPS and j == 0 and c + 2 < CHUNKS:
                load_chunk(c + 2)
            if 0 <= n + SQUARE_AHEAD < STEPS:
                square_step(n + SQUARE_AHEAD)
            if 0 <= n < STEPS:
                cube_step(n)
            if 0 <= n - 1 < STEPS and 1 <= (n - 1) % KNOTS <= LAST_THIRD:
                one_sided_step(n - 1)
            for half in HALVES[part]:
                base, r = divmod(half, MOST_ROW_TILES)
                for lag, step in ((BODY_LAG, body_step), (TAIL_LAG, tail_step)):
                    chunk, q = divmod(stage - lag, STAGES_A_CHUNK)
                    if 0 <= chunk < CHUNKS and r < ROW_TILES[chunk]:
                        step(chunk, q * BASES_A_STAGE + base, r)
            if 0 <= n < STEPS and j == 7:
                silu_chunk(c)
            if 2 <= n < 2 + PASSES:
                turn_weight_pass(n - 2)
            if n == KNOTS:
                quantise_weights()
            q = stage - BODY_LAG - 1
            if part == 1 and 0 <= q < stages and q % 2 == 1:
                quantise_group(q // STAGES_A_CHUNK, (q % STAGES_A_CHUNK) // 2)
            q = stage - BODY_LAG - 2
            if 0 <= q < stages and q % STAGES_A_CHUNK == STAGES_A_CHUNK - 1:
                if part == 0:
                    multiply_chunk(q // STAGES_A_CHUNK)
                if part == 2:
                    store_chunk(q // STAGES_A_CHUNK)
            if 0 <= n < STEPS and c + 1 < CHUNKS:
                if j == 5:
                    clamp_chunk(c + 1)
